import numpy as np
import ml_dtypes


def mxq(x, axis, fmt="e4m3"):
    dtype, down = {"e4m3": (ml_dtypes.float8_e4m3fn, 7), "e5m2": (ml_dtypes.float8_e5m2, 14)}[fmt]
    v = np.moveaxis(np.asarray(x, np.float32).astype(ml_dtypes.bfloat16).astype(np.float64), axis, -1)
    blocks = v.reshape(v.shape[:-1] + (-1, 32))
    amax = np.abs(blocks).max(-1, keepdims=True)
    byte = np.maximum(np.where(amax > 0, np.frexp(amax)[1] - 1 + 127, 0) - down, 1)
    scale = np.exp2(byte - 127.0)
    codes = (blocks / scale).astype(np.float32).astype(dtype).astype(np.float64)
    return np.moveaxis((codes * scale).reshape(v.shape), -1, axis)


WIDE = False


def mx_kscale(k):
    if not WIDE:
        return np.ones(k)
    levels = np.array([10, -10, 5, -5, 0])
    a = np.random.permutation(np.resize(levels, k // 512 * 4)).reshape(k // 512, 4)
    idx = np.arange(k)
    return np.exp2(a[idx // 512, idx % 128 // 32])


BF16 = ml_dtypes.bfloat16


def bf(x):
    return np.asarray(x, np.float32).astype(BF16)


def f64(x):
    return np.asarray(x).astype(np.float64)


B, S, D, NH, LAT, F = 4, 1024, 512, 16, 512, 8192
EPS = 1e-5


def layer_norm(c, g, b):
    m = c.mean(-1, keepdims=True)
    v = ((c - m) ** 2).mean(-1, keepdims=True)
    return (c - m) * (1.0 / np.sqrt(v + EPS)) * g + b


def down_weight():
    return (np.random.standard_normal((D, LAT)) + 0.3 * np.random.standard_normal((D, 1))) / np.sqrt(D)


def setup_inputs():
    s = mx_kscale(D)
    tq, tkv = mx_kscale(LAT), mx_kscale(LAT)
    return {
        "normed": bf(np.random.standard_normal((B, S, D)) * s),
        "W_dq": bf(down_weight() / s[:, None]),
        "q_ln_g": bf((1.0 + 0.1 * np.random.standard_normal(LAT)) * tq),
        "q_ln_b": bf(0.1 * np.random.standard_normal(LAT) * tq),
        "W_uq": bf(np.random.standard_normal((LAT, D)) / np.sqrt(LAT) / tq[:, None]),
        "W_dkv": bf(down_weight() / s[:, None]),
        "kv_ln_g": bf((1.0 + 0.1 * np.random.standard_normal(LAT)) * tkv),
        "kv_ln_b": bf(0.1 * np.random.standard_normal(LAT) * tkv),
        "W_ukv": bf(np.random.standard_normal((LAT, D + D)) / np.sqrt(LAT) / tkv[:, None]),
    }


def reference(normed, W_dq, q_ln_g, q_ln_b, W_uq, W_dkv, kv_ln_g, kv_ln_b, W_ukv):
    nq = mxq(f64(normed), 2, "e4m3")
    cq = layer_norm(nq @ mxq(f64(W_dq), 0, "e4m3"), f64(q_ln_g), f64(q_ln_b))
    Q = mxq(cq, 2, "e4m3") @ mxq(f64(W_uq), 0, "e4m3")
    ckv = layer_norm(nq @ mxq(f64(W_dkv), 0, "e4m3"), f64(kv_ln_g), f64(kv_ln_b))
    KV = mxq(ckv, 2, "e4m3") @ mxq(f64(W_ukv), 0, "e4m3")
    return Q, KV

@@ -1,0 +1,404 @@
+from contextlib import ExitStack
+
+import concourse.masks as masks
+import concourse.mybir as mybir
+
+F32 = mybir.dt.float32
+BF16 = mybir.dt.bfloat16
+U32 = mybir.dt.uint32
+U8 = mybir.dt.uint8
+FP8X4 = mybir.dt.float8_e4m3fn_x4
+ACT = mybir.ActivationFunctionType
+ALU = mybir.AluOpType
+
+P = 128
+PACK = 4
+FEATURES = 512
+LATENT = 512
+TOKENS = 4096
+TILES = 4
+GROUP = TILES * P
+GROUPS = TOKENS // GROUP
+HALF_TILES = TILES // 2
+HALF = HALF_TILES * P
+HALVES = 2 * GROUPS
+BANK = 512
+EPS = 1e-5
+BRANCHES = 2
+OUT_BANKS = (1, 2)
+UNITS = GROUPS * BRANCHES
+RING = 4
+FLOPS = 2 * TOKENS * 512 * (512 + 512 + 512 + 1024)
+
+
+def tile_transformerdecoderblock_pa_t_kernel(
+    tc, normed, W_dq, q_ln_g, q_ln_b, W_uq, W_dkv, kv_ln_g, kv_ln_b, W_ukv, out_0, out_1
+):
+    nc = tc.nc
+    down_w = (W_dq, W_dkv)
+    up_w = (W_uq, W_ukv)
+    gain_bias_vecs = ((q_ln_g, q_ln_b), (kv_ln_g, kv_ln_b))
+    x_view = normed.flatten_outer_dims().rearrange("(p s j) d -> s p j d", s=GROUPS, j=TILES)
+    out_views = (
+        out_0.flatten_outer_dims().rearrange("(p h j) d -> h p j d", h=HALVES, j=HALF_TILES),
+        out_1.flatten_outer_dims().rearrange("(p h j) d -> h p j d", h=HALVES, j=HALF_TILES),
+    )
+
+    with ExitStack() as stack:
+        consts = stack.enter_context(tc.tile_pool(name="consts", bufs=1))
+        wstage = stack.enter_context(tc.tile_pool(name="wstage", bufs=1))
+        xpool = stack.enter_context(tc.tile_pool(name="xpool", bufs=1))
+        npool = stack.enter_context(tc.tile_pool(name="npool", bufs=2))
+        small = stack.enter_context(tc.tile_pool(name="small", bufs=3))
+        work = stack.enter_context(tc.tile_pool(name="work", bufs=2))
+        opool = stack.enter_context(tc.tile_pool(name="opool", bufs=3))
+        ps_a = stack.enter_context(tc.psum_pool(name="ps_a", bufs=TILES))
+        ps_ring = stack.enter_context(tc.psum_pool(name="ps_ring", bufs=1))
+        stack.enter_context(tc.manual_schedule())
+
+        ring_count = [0]
+
+        def ring_bank(shape):
+            slot = ring_count[0] % RING
+            ring_count[0] += 1
+            return ps_ring.tile(shape, F32, name="ring%d" % slot)
+
+        gain_bias = consts.tile([P, BRANCHES, 2, PACK], F32, name="gain_bias")
+        vec_raws = []
+        for br in range(BRANCHES):
+            for v in range(2):
+                vec_raw = consts.tile([P, PACK], BF16, name="vec_raw%d%d" % (br, v))
+                nc.gpsimd.dma_start(
+                    out=vec_raw[:], in_=gain_bias_vecs[br][v].rearrange("(p t) -> p t", t=PACK)
+                )
+                vec_raws.append(vec_raw)
+
+        def load_down(br):
+            raw = wstage.tile([P, PACK, LATENT], BF16, name="down_raw%d" % br)
+            nc.sync.dma_start(
+                out=raw[:].rearrange("q (u e) c -> q u e c", u=2),
+                in_=down_w[br].rearrange("(u q e) c -> q u e c", u=2, e=2),
+            )
+            return raw
+
+        def load_tokens(s):
+            x = xpool.tile([P, TILES, FEATURES], BF16, name="x%d" % s)
+            nc.sync.dma_start(out=x[:], in_=x_view[s])
+            return x
+
+        def load_up(br):
+            raw = wstage.tile([P, PACK, OUT_BANKS[br] * BANK], BF16, name="up_raw%d" % br)
+            nc.sync.dma_start(out=raw[:], in_=up_w[br].rearrange("(p j) w -> p j w", j=PACK))
+            return raw
+
+        x_tiles = [load_tokens(0)]
+        down_raw = [load_down(br) for br in range(BRANCHES)]
+        x_tiles.append(load_tokens(1))
+        up_raw = [load_up(br) for br in range(BRANCHES)]
+        x_tiles.extend([load_tokens(s) for s in range(2, GROUPS)])
+
+        ident = consts.tile([P, P], F32, name="ident")
+        masks.make_identity(nc, ident[:])
+        eps_t = consts.tile([P, 1], F32, name="eps_t")
+        nc.vector.memset(eps_t[:], EPS)
+
+        def quantise_weight(grouped, width, name):
+            codes = consts.tile([P, width], U32, name=name + "_codes", align_bytes=64)
+            scales = consts.tile([P, width], U8, name=name + "_scales", align_bytes=64)
+            nc.vector.quantize_mx(
+                out=codes[:].bitcast(FP8X4),
+                scales=scales[:],
+                in_=grouped[:].rearrange("k c j -> k (c j)"),
+            )
+            return codes, scales
+
+        def regroup_down(br, copy):
+            grouped = wstage.tile([P, LATENT, PACK], BF16, name="down_grouped%d" % br, align_bytes=64)
+            copy(
+                out=grouped[:].rearrange("k (t p) j -> k t p j", t=PACK),
+                in_=down_raw[br][:].rearrange("k j (p t) -> k t p j", t=PACK),
+            )
+            return grouped
+
+        def regroup_up(br, copy):
+            width = OUT_BANKS[br] * BANK
+            grouped = wstage.tile([P, width, PACK], BF16, name="up_grouped%d" % br, align_bytes=64)
+            copy(
+                out=grouped[:].rearrange("p (c i) j -> p c j i", i=4),
+                in_=up_raw[br][:].rearrange("p j (c i) -> p c j i", i=4),
+            )
+            return grouped
+
+        n_grouped = {}
+        n_codes = {}
+        n_scales = {}
+
+        def transpose_tokens(half):
+            s, h = divmod(half, 2)
+            n_t = ring_bank([P, 2, HALF])
+            for jj in range(HALF_TILES):
+                x_words = x_tiles[s][:, HALF_TILES * h + jj, :].bitcast(F32)
+                for u in range(2):
+                    nc.tensor.transpose(
+                        n_t[:, u, jj * P : (jj + 1) * P], x_words[:, u * P : (u + 1) * P], ident[:]
+                    )
+            n_grouped[half] = npool.tile([P, HALF, PACK], BF16, name="n_grouped", align_bytes=64)
+            n_words = (
+                n_grouped[half][:]
+                .rearrange("p w j -> p (w j)")
+                .bitcast(F32)
+                .rearrange("p (w u) -> p w u", u=2)
+            )
+            nc.scalar.copy(out=n_words, in_=n_t[:].rearrange("p u w -> p w u"))
+
+        def quantise_tokens(half):
+            s, h = divmod(half, 2)
+            if h == 0:
+                n_codes[s] = npool.tile([P, GROUP], U32, name="n_codes", align_bytes=64)
+                n_scales[s] = npool.tile([P, GROUP], U8, name="n_scales", align_bytes=64)
+            nc.vector.quantize_mx(
+                out=n_codes[s][:, h * HALF : (h + 1) * HALF].bitcast(FP8X4),
+                scales=n_scales[s][:, h * HALF : (h + 1) * HALF],
+                in_=n_grouped[half][:].rearrange("p w j -> p (w j)"),
+            )
+
+        sums = {}
+        stats = {}
+        mean_var = {}
+        rstd = {}
+        shift = {}
+        xhat = {}
+        planes = {}
+        c_grouped = {}
+        c_codes = {}
+        c_scales = {}
+
+        def down_matmul(unit, j):
+            s, br = divmod(unit, BRANCHES)
+            sums[unit, j] = ps_a.tile([P, LATENT], F32, name="sums")
+            nc.tensor.matmul_mx(
+                out=sums[unit, j][:],
+                lhsT=n_codes[s][:, j * P : (j + 1) * P].bitcast(FP8X4),
+                lhsT_scale=n_scales[s][:, j * P : (j + 1) * P],
+                rhs=down_codes[br][:].bitcast(FP8X4),
+                rhs_scale=down_scales[br][:],
+                start=True,
+                stop=True,
+            )
+
+        def token_stats(unit, j):
+            if j == 0:
+                stats[unit] = small.tile([P, TILES, 6], F32, name="stats")
+                mean_var[unit] = small.tile([P, TILES, 2], F32, name="mean_var")
+            nc.vector.bn_stats(out=stats[unit][:, j, :], in_=sums[unit, j][:])
+            nc.vector.bn_aggr(out=mean_var[unit][:, j, :], in_=stats[unit][:, j, :])
+
+        def std_of(unit):
+            std = small.tile([P, TILES], F32, name="std")
+            nc.scalar.activation(
+                out=std[:], in_=mean_var[unit][:, :, 1], func=ACT.Sqrt, bias=eps_t[:], scale=1.0
+            )
+            return std
+
+        def scale_and_shift(unit, std):
+            rstd[unit] = small.tile([P, TILES], F32, name="rstd")
+            nc.vector.reciprocal(out=rstd[unit][:], in_=std[:])
+            shift[unit] = small.tile([P, TILES], F32, name="shift")
+            nc.vector.scalar_tensor_tensor(
+                out=shift[unit][:],
+                in0=mean_var[unit][:, :, 0],
+                scalar=-1.0,
+                in1=rstd[unit][:],
+                op0=ALU.mult,
+                op1=ALU.mult,
+            )
+
+        def normalise(unit, j, on_vector):
+            if j == 0:
+                xhat[unit] = work.tile([P, TILES, LATENT], F32, name="xhat")
+            if on_vector:
+                nc.vector.tensor_scalar(
+                    out=xhat[unit][:, j, :],
+                    in0=sums[unit, j][:],
+                    scalar1=rstd[unit][:, j : j + 1],
+                    scalar2=shift[unit][:, j : j + 1],
+                    op0=ALU.mult,
+                    op1=ALU.add,
+                )
+            else:
+                nc.scalar.activation(
+                    out=xhat[unit][:, j, :],
+                    in_=sums[unit, j][:],
+                    func=ACT.Identity,
+                    scale=rstd[unit][:, j : j + 1],
+                    bias=shift[unit][:, j : j + 1],
+                )
+
+        def transpose_latent(unit, t):
+            x_t = ring_bank([P, GROUP])
+            for j in range(TILES):
+                nc.tensor.transpose(
+                    x_t[:, j * P : (j + 1) * P], xhat[unit][:, j, t * P : (t + 1) * P], ident[:]
+                )
+            return x_t
+
+        def gain_and_bias(unit, t, x_t, on_vector):
+            br = unit % BRANCHES
+            if t == 0:
+                planes[unit] = work.tile([P, PACK, GROUP], BF16, name="planes")
+            if on_vector:
+                nc.vector.tensor_scalar(
+                    out=planes[unit][:, t, :],
+                    in0=x_t[:],
+                    scalar1=gain_bias[:, br, 0, t : t + 1],
+                    scalar2=gain_bias[:, br, 1, t : t + 1],
+                    op0=ALU.mult,
+                    op1=ALU.add,
+                )
+            else:
+                nc.scalar.activation(
+                    out=planes[unit][:, t, :],
+                    in_=x_t[:],
+                    func=ACT.Identity,
+                    scale=gain_bias[:, br, 0, t : t + 1],
+                    bias=gain_bias[:, br, 1, t : t + 1],
+                )
+
+        def regroup_latent(unit):
+            c_grouped[unit] = work.tile([P, GROUP, PACK], BF16, name="c_grouped", align_bytes=64)
+            nc.vector.tensor_copy(
+                out=c_grouped[unit][:].rearrange("p (c i) t -> p c t i", i=4),
+                in_=planes[unit][:].rearrange("p t (c i) -> p c t i", i=4),
+            )
+
+        def quantise_latent(unit):
+            br = unit % BRANCHES
+            c_codes[unit] = work.tile([P, GROUP], U32, name="c_codes%d" % br, align_bytes=64)
+            c_scales[unit] = work.tile([P, GROUP], U8, name="c_scales%d" % br, align_bytes=64)
+            nc.vector.quantize_mx(
+                out=c_codes[unit][:].bitcast(FP8X4),
+                scales=c_scales[unit][:],
+                in_=c_grouped[unit][:].rearrange("p w t -> p (w t)"),
+            )
+
+        results = {}
+
+        def up_matmul(half, bank):
+            s, h = divmod(half, 2)
+            jj, col = divmod(bank, 3)
+            br = min(col, 1)
+            n = col - br
+            j = HALF_TILES * h + jj
+            unit = s * BRANCHES + br
+            acc = ring_bank([P, BANK])
+            nc.tensor.matmul_mx(
+                out=acc[:],
+                lhsT=c_codes[unit][:, j * P : (j + 1) * P].bitcast(FP8X4),
+                lhsT_scale=c_scales[unit][:, j * P : (j + 1) * P],
+                rhs=up_codes[br][:, n * BANK : (n + 1) * BANK].bitcast(FP8X4),
+                rhs_scale=up_scales[br][:, n * BANK : (n + 1) * BANK],
+                start=True,
+                stop=True,
+            )
+            return acc
+
+        def result_slice(half, bank):
+            jj, col = divmod(bank, 3)
+            br = min(col, 1)
+            n = col - br
+            if bank == 0:
+                for b in range(BRANCHES):
+                    results[half, b] = opool.tile(
+                        [P, HALF_TILES, OUT_BANKS[b] * BANK], F32, name="result%d" % b
+                    )
+            return results[half, br][:, jj, n * BANK : (n + 1) * BANK]
+
+        def store(half):
+            for br in range(BRANCHES):
+                nc.sync.dma_start(out=out_views[br][half], in_=results[half, br][:])
+
+        acc = {}
+
+        def drain(half, bank):
+            if bank % 2 == 0:
+                nc.vector.tensor_copy(out=result_slice(half, bank), in_=acc[half, bank][:])
+            else:
+                nc.scalar.copy(out=result_slice(half, bank), in_=acc[half, bank][:])
+
+        transpose_tokens(0)
+        transpose_tokens(1)
+        down_grouped = [regroup_down(0, nc.vector.tensor_copy), regroup_down(1, nc.scalar.copy)]
+        up_grouped = [regroup_up(0, nc.scalar.copy)]
+        quantise_tokens(0)
+        down_codes = []
+        down_scales = []
+        codes, scales = quantise_weight(down_grouped[0], LATENT, "down0")
+        down_codes.append(codes)
+        down_scales.append(scales)
+        quantise_tokens(1)
+        up_codes = []
+        up_scales = []
+
+        for k in range(UNITS + 3):
+            front = k if k < UNITS else None
+            mid = k - 1 if 0 <= k - 1 < UNITS else None
+            late = k - 2 if 0 <= k - 2 < UNITS else None
+            back = k - 3 if 0 <= k - 3 < HALVES else None
+            ahead = k + 2 if k + 2 < HALVES else None
+            share = front is None
+
+            if late is not None:
+                quantise_latent(late)
+            if 2 <= k + 1 < HALVES:
+                quantise_tokens(k + 1)
+            if back is not None:
+                drain(back, 0)
+            for j in range(TILES):
+                if mid is not None:
+                    normalise(mid, j, share and j % 2 == 1)
+                if front is not None:
+                    down_matmul(front, j)
+                    token_stats(front, j)
+                if back is not None and j < 2:
+                    acc[back, 1 + j] = up_matmul(back, 1 + j)
+                if back is not None and j == 1:
+                    drain(back, 2)
+            if back is not None:
+                drain(back, 3)
+                drain(back, 1)
+            if front is not None and mid is None:
+                std = std_of(front)
+            if mid is not None:
+                for t in range(PACK):
+                    x_t = transpose_latent(mid, t)
+                    gain_and_bias(mid, t, x_t, share and t % 2 == 1)
+                    if t == 2 and front is not None:
+                        std = std_of(front)
+            if ahead is not None:
+                transpose_tokens(ahead)
+            if back is not None:
+                acc[back, 4] = up_matmul(back, 4)
+                acc[back, 5] = up_matmul(back, 5)
+                drain(back, 4)
+            if front is not None:
+                scale_and_shift(front, std)
+            if k == 0:
+                codes, scales = quantise_weight(down_grouped[1], LATENT, "down1")
+                down_codes.append(codes)
+                down_scales.append(scales)
+                for i in range(BRANCHES * 2):
+                    nc.vector.tensor_copy(out=gain_bias[:, i // 2, i % 2, :], in_=vec_raws[i][:])
+                up_grouped.append(regroup_up(1, nc.vector.tensor_copy))
+            if k == 1:
+                for br in range(BRANCHES):
+                    codes, scales = quantise_weight(up_grouped[br], OUT_BANKS[br] * BANK, "up%d" % br)
+                    up_codes.append(codes)
+                    up_scales.append(scales)
+            if mid is not None:
+                regroup_latent(mid)
+            if back is not None:
+                drain(back, 5)
+                store(back)
+            if 0 <= k - 2 < HALVES:
+                acc[k - 2, 0] = up_matmul(k - 2, 0)
+                acc[k - 2, 3] = up_matmul(k - 2, 3)

@@ -25,9 +25,9 @@ HALVES = 2 * GROUPS
 BANK = 512
 EPS = 1e-5
 BRANCHES = 2
-OUT_BANKS = (1, 2)
+OUT_BANKS = (2, 1)
 UNITS = GROUPS * BRANCHES
-RING = 4
+RING = 8
 FLOPS = 2 * TOKENS * 512 * (512 + 512 + 512 + 1024)
 
 
@@ -35,13 +35,13 @@ def tile_transformerdecoderblock_pa_t_kernel(
     tc, normed, W_dq, q_ln_g, q_ln_b, W_uq, W_dkv, kv_ln_g, kv_ln_b, W_ukv, out_0, out_1
 ):
     nc = tc.nc
-    down_w = (W_dq, W_dkv)
-    up_w = (W_uq, W_ukv)
-    gain_bias_vecs = ((q_ln_g, q_ln_b), (kv_ln_g, kv_ln_b))
+    down_w = (W_dkv, W_dq)
+    up_w = (W_ukv, W_uq)
+    gain_bias_vecs = ((kv_ln_g, kv_ln_b), (q_ln_g, q_ln_b))
     x_view = normed.flatten_outer_dims().rearrange("(p s j) d -> s p j d", s=GROUPS, j=TILES)
     out_views = (
-        out_0.flatten_outer_dims().rearrange("(p h j) d -> h p j d", h=HALVES, j=HALF_TILES),
         out_1.flatten_outer_dims().rearrange("(p h j) d -> h p j d", h=HALVES, j=HALF_TILES),
+        out_0.flatten_outer_dims().rearrange("(p h j) d -> h p j d", h=HALVES, j=HALF_TILES),
     )
 
     with ExitStack() as stack:
@@ -50,9 +50,9 @@ def tile_transformerdecoderblock_pa_t_kernel(
         xpool = stack.enter_context(tc.tile_pool(name="xpool", bufs=1))
         npool = stack.enter_context(tc.tile_pool(name="npool", bufs=2))
         small = stack.enter_context(tc.tile_pool(name="small", bufs=3))
+        latent = stack.enter_context(tc.tile_pool(name="latent", bufs=3))
         work = stack.enter_context(tc.tile_pool(name="work", bufs=2))
         opool = stack.enter_context(tc.tile_pool(name="opool", bufs=3))
-        ps_a = stack.enter_context(tc.psum_pool(name="ps_a", bufs=TILES))
         ps_ring = stack.enter_context(tc.psum_pool(name="ps_ring", bufs=1))
         stack.enter_context(tc.manual_schedule())
 
@@ -63,12 +63,17 @@ def tile_transformerdecoderblock_pa_t_kernel(
             ring_count[0] += 1
             return ps_ring.tile(shape, F32, name="ring%d" % slot)
 
+        ident = consts.tile([P, P], F32, name="ident")
+        masks.make_identity(nc, ident[:])
+        eps_t = consts.tile([P, 1], F32, name="eps_t")
+        nc.vector.memset(eps_t[:], EPS)
+
         gain_bias = consts.tile([P, BRANCHES, 2, PACK], F32, name="gain_bias")
         vec_raws = []
         for br in range(BRANCHES):
             for v in range(2):
                 vec_raw = consts.tile([P, PACK], BF16, name="vec_raw%d%d" % (br, v))
-                nc.gpsimd.dma_start(
+                nc.scalar.dma_start(
                     out=vec_raw[:], in_=gain_bias_vecs[br][v].rearrange("(p t) -> p t", t=PACK)
                 )
                 vec_raws.append(vec_raw)
@@ -96,11 +101,6 @@ def tile_transformerdecoderblock_pa_t_kernel(
         x_tiles.append(load_tokens(1))
         up_raw = [load_up(br) for br in range(BRANCHES)]
         x_tiles.extend([load_tokens(s) for s in range(2, GROUPS)])
-
-        ident = consts.tile([P, P], F32, name="ident")
-        masks.make_identity(nc, ident[:])
-        eps_t = consts.tile([P, 1], F32, name="eps_t")
-        nc.vector.memset(eps_t[:], EPS)
 
         def quantise_weight(grouped, width, name):
             codes = consts.tile([P, width], U32, name=name + "_codes", align_bytes=64)
@@ -142,6 +142,9 @@ def tile_transformerdecoderblock_pa_t_kernel(
                     nc.tensor.transpose(
                         n_t[:, u, jj * P : (jj + 1) * P], x_words[:, u * P : (u + 1) * P], ident[:]
                     )
+            return n_t
+
+        def copy_tokens(half, n_t):
             n_grouped[half] = npool.tile([P, HALF, PACK], BF16, name="n_grouped", align_bytes=64)
             n_words = (
                 n_grouped[half][:]
@@ -162,12 +165,11 @@ def tile_transformerdecoderblock_pa_t_kernel(
                 in_=n_grouped[half][:].rearrange("p w j -> p (w j)"),
             )
 
-        sums = {}
+        c_f32 = {}
         stats = {}
         mean_var = {}
         rstd = {}
         shift = {}
-        xhat = {}
         planes = {}
         c_grouped = {}
         c_codes = {}
@@ -175,9 +177,9 @@ def tile_transformerdecoderblock_pa_t_kernel(
 
         def down_matmul(unit, j):
             s, br = divmod(unit, BRANCHES)
-            sums[unit, j] = ps_a.tile([P, LATENT], F32, name="sums")
+            sums = ring_bank([P, LATENT])
             nc.tensor.matmul_mx(
-                out=sums[unit, j][:],
+                out=sums[:],
                 lhsT=n_codes[s][:, j * P : (j + 1) * P].bitcast(FP8X4),
                 lhsT_scale=n_scales[s][:, j * P : (j + 1) * P],
                 rhs=down_codes[br][:].bitcast(FP8X4),
@@ -185,12 +187,18 @@ def tile_transformerdecoderblock_pa_t_kernel(
                 start=True,
                 stop=True,
             )
+            return sums
+
+        def copy_sums(unit, j, sums):
+            if j == 0:
+                c_f32[unit] = latent.tile([P, TILES, LATENT], F32, name="c_f32")
+            nc.scalar.copy(out=c_f32[unit][:, j, :], in_=sums[:])
 
         def token_stats(unit, j):
             if j == 0:
                 stats[unit] = small.tile([P, TILES, 6], F32, name="stats")
                 mean_var[unit] = small.tile([P, TILES, 2], F32, name="mean_var")
-            nc.vector.bn_stats(out=stats[unit][:, j, :], in_=sums[unit, j][:])
+            nc.vector.bn_stats(out=stats[unit][:, j, :], in_=c_f32[unit][:, j, :])
             nc.vector.bn_aggr(out=mean_var[unit][:, j, :], in_=stats[unit][:, j, :])
 
         def std_of(unit):
@@ -213,32 +221,21 @@ def tile_transformerdecoderblock_pa_t_kernel(
                 op1=ALU.mult,
             )
 
-        def normalise(unit, j, on_vector):
-            if j == 0:
-                xhat[unit] = work.tile([P, TILES, LATENT], F32, name="xhat")
-            if on_vector:
-                nc.vector.tensor_scalar(
-                    out=xhat[unit][:, j, :],
-                    in0=sums[unit, j][:],
-                    scalar1=rstd[unit][:, j : j + 1],
-                    scalar2=shift[unit][:, j : j + 1],
-                    op0=ALU.mult,
-                    op1=ALU.add,
-                )
-            else:
-                nc.scalar.activation(
-                    out=xhat[unit][:, j, :],
-                    in_=sums[unit, j][:],
-                    func=ACT.Identity,
-                    scale=rstd[unit][:, j : j + 1],
-                    bias=shift[unit][:, j : j + 1],
-                )
+        def normalise(unit, j, engine):
+            engine.tensor_scalar(
+                out=c_f32[unit][:, j, :],
+                in0=c_f32[unit][:, j, :],
+                scalar1=rstd[unit][:, j : j + 1],
+                scalar2=shift[unit][:, j : j + 1],
+                op0=ALU.mult,
+                op1=ALU.add,
+            )
 
         def transpose_latent(unit, t):
             x_t = ring_bank([P, GROUP])
             for j in range(TILES):
                 nc.tensor.transpose(
-                    x_t[:, j * P : (j + 1) * P], xhat[unit][:, j, t * P : (t + 1) * P], ident[:]
+                    x_t[:, j * P : (j + 1) * P], c_f32[unit][:, j, t * P : (t + 1) * P], ident[:]
                 )
             return x_t
 
@@ -281,15 +278,8 @@ def tile_transformerdecoderblock_pa_t_kernel(
                 in_=c_grouped[unit][:].rearrange("p w t -> p (w t)"),
             )
 
-        results = {}
-
-        def up_matmul(half, bank):
-            s, h = divmod(half, 2)
-            jj, col = divmod(bank, 3)
-            br = min(col, 1)
-            n = col - br
-            j = HALF_TILES * h + jj
-            unit = s * BRANCHES + br
+        def up_matmul(unit, j, n):
+            br = unit % BRANCHES
             acc = ring_bank([P, BANK])
             nc.tensor.matmul_mx(
                 out=acc[:],
@@ -302,103 +292,80 @@ def tile_transformerdecoderblock_pa_t_kernel(
             )
             return acc
 
-        def result_slice(half, bank):
-            jj, col = divmod(bank, 3)
-            br = min(col, 1)
-            n = col - br
-            if bank == 0:
-                for b in range(BRANCHES):
-                    results[half, b] = opool.tile(
-                        [P, HALF_TILES, OUT_BANKS[b] * BANK], F32, name="result%d" % b
-                    )
-            return results[half, br][:, jj, n * BANK : (n + 1) * BANK]
+        def up_and_store(unit):
+            s, br = divmod(unit, BRANCHES)
+            bank = 0
+            for h in range(2):
+                result = opool.tile([P, HALF_TILES, OUT_BANKS[br] * BANK], F32, name="result%d" % br)
+                for jj in range(HALF_TILES):
+                    for n in range(OUT_BANKS[br]):
+                        acc = up_matmul(unit, h * HALF_TILES + jj, n)
+                        if bank % 2 == 0:
+                            nc.vector.tensor_copy(out=result[:, jj, n * BANK : (n + 1) * BANK], in_=acc[:])
+                        else:
+                            nc.scalar.copy(out=result[:, jj, n * BANK : (n + 1) * BANK], in_=acc[:])
+                        bank += 1
+                nc.sync.dma_start(out=out_views[br][2 * s + h], in_=result[:])
 
-        def store(half):
-            for br in range(BRANCHES):
-                nc.sync.dma_start(out=out_views[br][half], in_=results[half, br][:])
-
-        acc = {}
-
-        def drain(half, bank):
-            if bank % 2 == 0:
-                nc.vector.tensor_copy(out=result_slice(half, bank), in_=acc[half, bank][:])
-            else:
-                nc.scalar.copy(out=result_slice(half, bank), in_=acc[half, bank][:])
-
-        transpose_tokens(0)
-        transpose_tokens(1)
+        for half in range(2):
+            copy_tokens(half, transpose_tokens(half))
         down_grouped = [regroup_down(0, nc.vector.tensor_copy), regroup_down(1, nc.scalar.copy)]
-        up_grouped = [regroup_up(0, nc.scalar.copy)]
         quantise_tokens(0)
         down_codes = []
         down_scales = []
+        up_codes = []
+        up_scales = []
         codes, scales = quantise_weight(down_grouped[0], LATENT, "down0")
         down_codes.append(codes)
         down_scales.append(scales)
         quantise_tokens(1)
-        up_codes = []
-        up_scales = []
+        codes, scales = quantise_weight(down_grouped[1], LATENT, "down1")
+        down_codes.append(codes)
+        down_scales.append(scales)
+
+        def unit_or_none(u):
+            return u if 0 <= u < UNITS else None
 
         for k in range(UNITS + 3):
-            front = k if k < UNITS else None
-            mid = k - 1 if 0 <= k - 1 < UNITS else None
-            late = k - 2 if 0 <= k - 2 < UNITS else None
-            back = k - 3 if 0 <= k - 3 < HALVES else None
-            ahead = k + 2 if k + 2 < HALVES else None
-            share = front is None
+            first = unit_or_none(k)
+            second = unit_or_none(k - 1)
+            third = unit_or_none(k - 2)
+            fourth = unit_or_none(k - 3)
+            vector_free = first is None
 
-            if late is not None:
-                quantise_latent(late)
-            if 2 <= k + 1 < HALVES:
-                quantise_tokens(k + 1)
-            if back is not None:
-                drain(back, 0)
+            if fourth is not None:
+                regroup_latent(fourth)
+            if 1 <= k and k + 2 < HALVES:
+                quantise_tokens(k + 2)
+            if fourth is not None:
+                quantise_latent(fourth)
             for j in range(TILES):
-                if mid is not None:
-                    normalise(mid, j, share and j % 2 == 1)
-                if front is not None:
-                    down_matmul(front, j)
-                    token_stats(front, j)
-                if back is not None and j < 2:
-                    acc[back, 1 + j] = up_matmul(back, 1 + j)
-                if back is not None and j == 1:
-                    drain(back, 2)
-            if back is not None:
-                drain(back, 3)
-                drain(back, 1)
-            if front is not None and mid is None:
-                std = std_of(front)
-            if mid is not None:
-                for t in range(PACK):
-                    x_t = transpose_latent(mid, t)
-                    gain_and_bias(mid, t, x_t, share and t % 2 == 1)
-                    if t == 2 and front is not None:
-                        std = std_of(front)
-            if ahead is not None:
-                transpose_tokens(ahead)
-            if back is not None:
-                acc[back, 4] = up_matmul(back, 4)
-                acc[back, 5] = up_matmul(back, 5)
-                drain(back, 4)
-            if front is not None:
-                scale_and_shift(front, std)
+                if first is not None:
+                    copy_sums(first, j, down_matmul(first, j))
+                if j == 1 and second is not None:
+                    scale_and_shift(second, std_of(second))
+            if second is not None:
+                for j in range(TILES):
+                    normalise(second, j, nc.vector if vector_free else nc.gpsimd)
+            if first is not None:
+                for j in range(TILES):
+                    token_stats(first, j)
             if k == 0:
-                codes, scales = quantise_weight(down_grouped[1], LATENT, "down1")
-                down_codes.append(codes)
-                down_scales.append(scales)
+                copy_tokens(2, transpose_tokens(2))
+                quantise_tokens(2)
                 for i in range(BRANCHES * 2):
                     nc.vector.tensor_copy(out=gain_bias[:, i // 2, i % 2, :], in_=vec_raws[i][:])
-                up_grouped.append(regroup_up(1, nc.vector.tensor_copy))
-            if k == 1:
-                for br in range(BRANCHES):
-                    codes, scales = quantise_weight(up_grouped[br], OUT_BANKS[br] * BANK, "up%d" % br)
-                    up_codes.append(codes)
-                    up_scales.append(scales)
-            if mid is not None:
-                regroup_latent(mid)
-            if back is not None:
-                drain(back, 5)
-                store(back)
-            if 0 <= k - 2 < HALVES:
-                acc[k - 2, 0] = up_matmul(k - 2, 0)
-                acc[k - 2, 3] = up_matmul(k - 2, 3)
+            if k == 1 or k == 2:
+                br = k - 1
+                codes, scales = quantise_weight(
+                    regroup_up(br, nc.vector.tensor_copy), OUT_BANKS[br] * BANK, "up%d" % br
+                )
+                up_codes.append(codes)
+                up_scales.append(scales)
+            if third is not None:
+                for t in range(PACK):
+                    gain_and_bias(third, t, transpose_latent(third, t), vector_free and t % 2 == 1)
+            if k + 3 < HALVES:
+                copy_tokens(k + 3, transpose_tokens(k + 3))
+            if fourth is not None:
+                up_and_store(fourth)

@@ -65,18 +65,18 @@ def tile_transformerdecoderblock_pa_t_kernel(
 
         ident = consts.tile([P, P], F32, name="ident")
         masks.make_identity(nc, ident[:])
-        eps_t = consts.tile([P, 1], F32, name="eps_t")
-        nc.vector.memset(eps_t[:], EPS)
 
         gain_bias = consts.tile([P, BRANCHES, 2, PACK], F32, name="gain_bias")
-        vec_raws = []
+        vec_raw = consts.tile([P, BRANCHES, 2, 16], BF16, name="vec_raw")
         for br in range(BRANCHES):
             for v in range(2):
-                vec_raw = consts.tile([P, PACK], BF16, name="vec_raw%d%d" % (br, v))
                 nc.scalar.dma_start(
-                    out=vec_raw[:], in_=gain_bias_vecs[br][v].rearrange("(p t) -> p t", t=PACK)
+                    out=vec_raw[:, br, v, 0:PACK],
+                    in_=gain_bias_vecs[br][v].rearrange("(p t) -> p t", t=PACK),
                 )
-                vec_raws.append(vec_raw)
+        nc.gpsimd.tensor_copy(out=gain_bias[:], in_=vec_raw[:, :, :, 0:PACK])
+        neg_half = consts.tile([P, TILES], F32, name="neg_half")
+        nc.gpsimd.memset(neg_half[:], -0.5)
 
         def load_down(br):
             raw = wstage.tile([P, PACK, LATENT], BF16, name="down_raw%d" % br)
@@ -145,31 +145,31 @@ def tile_transformerdecoderblock_pa_t_kernel(
             return n_t
 
         def copy_tokens(half, n_t):
-            n_grouped[half] = npool.tile([P, HALF, PACK], BF16, name="n_grouped", align_bytes=64)
+            s, h = divmod(half, 2)
+            if h == 0:
+                n_grouped[s] = npool.tile([P, GROUP, PACK], BF16, name="n_grouped", align_bytes=64)
             n_words = (
-                n_grouped[half][:]
+                n_grouped[s][:, h * HALF : (h + 1) * HALF, :]
                 .rearrange("p w j -> p (w j)")
                 .bitcast(F32)
                 .rearrange("p (w u) -> p w u", u=2)
             )
             nc.scalar.copy(out=n_words, in_=n_t[:].rearrange("p u w -> p w u"))
 
-        def quantise_tokens(half):
-            s, h = divmod(half, 2)
-            if h == 0:
-                n_codes[s] = npool.tile([P, GROUP], U32, name="n_codes", align_bytes=64)
-                n_scales[s] = npool.tile([P, GROUP], U8, name="n_scales", align_bytes=64)
+        def quantise_tokens(s):
+            n_codes[s] = npool.tile([P, GROUP], U32, name="n_codes", align_bytes=64)
+            n_scales[s] = npool.tile([P, GROUP], U8, name="n_scales", align_bytes=64)
             nc.vector.quantize_mx(
-                out=n_codes[s][:, h * HALF : (h + 1) * HALF].bitcast(FP8X4),
-                scales=n_scales[s][:, h * HALF : (h + 1) * HALF],
-                in_=n_grouped[half][:].rearrange("p w j -> p (w j)"),
+                out=n_codes[s][:].bitcast(FP8X4),
+                scales=n_scales[s][:],
+                in_=n_grouped[s][:].rearrange("p w j -> p (w j)"),
             )
 
         c_f32 = {}
         stats = {}
         mean_var = {}
         rstd = {}
-        shift = {}
+        neg_mean = {}
         planes = {}
         c_grouped = {}
         c_codes = {}
@@ -201,34 +201,28 @@ def tile_transformerdecoderblock_pa_t_kernel(
             nc.vector.bn_stats(out=stats[unit][:, j, :], in_=c_f32[unit][:, j, :])
             nc.vector.bn_aggr(out=mean_var[unit][:, j, :], in_=stats[unit][:, j, :])
 
-        def std_of(unit):
-            std = small.tile([P, TILES], F32, name="std")
-            nc.scalar.activation(
-                out=std[:], in_=mean_var[unit][:, :, 1], func=ACT.Sqrt, bias=eps_t[:], scale=1.0
+        def reciprocal_std(unit):
+            var_eps = small.tile([P, TILES], F32, name="var_eps")
+            nc.gpsimd.tensor_scalar(
+                out=var_eps[:], in0=mean_var[unit][:, :, 1], scalar1=1.0, scalar2=EPS, op0=ALU.mult, op1=ALU.add
             )
-            return std
-
-        def scale_and_shift(unit, std):
             rstd[unit] = small.tile([P, TILES], F32, name="rstd")
-            nc.vector.reciprocal(out=rstd[unit][:], in_=std[:])
-            shift[unit] = small.tile([P, TILES], F32, name="shift")
-            nc.vector.scalar_tensor_tensor(
-                out=shift[unit][:],
-                in0=mean_var[unit][:, :, 0],
-                scalar=-1.0,
-                in1=rstd[unit][:],
-                op0=ALU.mult,
-                op1=ALU.mult,
+            nc.gpsimd.tensor_tensor(out=rstd[unit][:], in0=var_eps[:], in1=neg_half[:], op=ALU.pow)
+
+        def negative_mean(unit):
+            neg_mean[unit] = small.tile([P, TILES], F32, name="neg_mean")
+            nc.vector.tensor_scalar(
+                out=neg_mean[unit][:], in0=mean_var[unit][:, :, 0], scalar1=-1.0, scalar2=None, op0=ALU.mult
             )
 
         def normalise(unit, j, engine):
             engine.tensor_scalar(
                 out=c_f32[unit][:, j, :],
                 in0=c_f32[unit][:, j, :],
-                scalar1=rstd[unit][:, j : j + 1],
-                scalar2=shift[unit][:, j : j + 1],
-                op0=ALU.mult,
-                op1=ALU.add,
+                scalar1=neg_mean[unit][:, j : j + 1],
+                scalar2=rstd[unit][:, j : j + 1],
+                op0=ALU.add,
+                op1=ALU.mult,
             )
 
         def transpose_latent(unit, t):
@@ -239,27 +233,17 @@ def tile_transformerdecoderblock_pa_t_kernel(
                 )
             return x_t
 
-        def gain_and_bias(unit, t, x_t, on_vector):
+        def gain_and_bias(unit, t, x_t):
             br = unit % BRANCHES
             if t == 0:
                 planes[unit] = work.tile([P, PACK, GROUP], BF16, name="planes")
-            if on_vector:
-                nc.vector.tensor_scalar(
-                    out=planes[unit][:, t, :],
-                    in0=x_t[:],
-                    scalar1=gain_bias[:, br, 0, t : t + 1],
-                    scalar2=gain_bias[:, br, 1, t : t + 1],
-                    op0=ALU.mult,
-                    op1=ALU.add,
-                )
-            else:
-                nc.scalar.activation(
-                    out=planes[unit][:, t, :],
-                    in_=x_t[:],
-                    func=ACT.Identity,
-                    scale=gain_bias[:, br, 0, t : t + 1],
-                    bias=gain_bias[:, br, 1, t : t + 1],
-                )
+            nc.scalar.activation(
+                out=planes[unit][:, t, :],
+                in_=x_t[:],
+                func=ACT.Identity,
+                scale=gain_bias[:, br, 0, t : t + 1],
+                bias=gain_bias[:, br, 1, t : t + 1],
+            )
 
         def regroup_latent(unit):
             c_grouped[unit] = work.tile([P, GROUP, PACK], BF16, name="c_grouped", align_bytes=64)
@@ -315,13 +299,10 @@ def tile_transformerdecoderblock_pa_t_kernel(
         down_scales = []
         up_codes = []
         up_scales = []
-        codes, scales = quantise_weight(down_grouped[0], LATENT, "down0")
-        down_codes.append(codes)
-        down_scales.append(scales)
-        quantise_tokens(1)
-        codes, scales = quantise_weight(down_grouped[1], LATENT, "down1")
-        down_codes.append(codes)
-        down_scales.append(scales)
+        for br in range(BRANCHES):
+            codes, scales = quantise_weight(down_grouped[br], LATENT, "down%d" % br)
+            down_codes.append(codes)
+            down_scales.append(scales)
 
         def unit_or_none(u):
             return u if 0 <= u < UNITS else None
@@ -335,26 +316,20 @@ def tile_transformerdecoderblock_pa_t_kernel(
 
             if fourth is not None:
                 regroup_latent(fourth)
-            if 1 <= k and k + 2 < HALVES:
-                quantise_tokens(k + 2)
+            if k % 2 == 1 and (k + 1) // 2 < GROUPS:
+                quantise_tokens((k + 1) // 2)
             if fourth is not None:
                 quantise_latent(fourth)
-            for j in range(TILES):
-                if first is not None:
-                    copy_sums(first, j, down_matmul(first, j))
-                if j == 1 and second is not None:
-                    scale_and_shift(second, std_of(second))
             if second is not None:
+                negative_mean(second)
                 for j in range(TILES):
                     normalise(second, j, nc.vector if vector_free else nc.gpsimd)
             if first is not None:
                 for j in range(TILES):
+                    copy_sums(first, j, down_matmul(first, j))
+                for j in range(TILES):
                     token_stats(first, j)
-            if k == 0:
-                copy_tokens(2, transpose_tokens(2))
-                quantise_tokens(2)
-                for i in range(BRANCHES * 2):
-                    nc.vector.tensor_copy(out=gain_bias[:, i // 2, i % 2, :], in_=vec_raws[i][:])
+                reciprocal_std(first)
             if k == 1 or k == 2:
                 br = k - 1
                 codes, scales = quantise_weight(
@@ -364,7 +339,9 @@ def tile_transformerdecoderblock_pa_t_kernel(
                 up_scales.append(scales)
             if third is not None:
                 for t in range(PACK):
-                    gain_and_bias(third, t, transpose_latent(third, t), vector_free and t % 2 == 1)
+                    gain_and_bias(third, t, transpose_latent(third, t))
+            if k == 0:
+                copy_tokens(2, transpose_tokens(2))
             if k + 3 < HALVES:
                 copy_tokens(k + 3, transpose_tokens(k + 3))
             if fourth is not None:

@@ -27,7 +27,8 @@ EPS = 1e-5
 BRANCHES = 2
 OUT_BANKS = (2, 1)
 UNITS = GROUPS * BRANCHES
-RING = 8
+RING = 4
+PERIOD_BANKS = 6
 FLOPS = 2 * TOKENS * 512 * (512 + 512 + 512 + 1024)
 
 
@@ -51,9 +52,9 @@ def tile_transformerdecoderblock_pa_t_kernel(
         npool = stack.enter_context(tc.tile_pool(name="npool", bufs=2))
         small = stack.enter_context(tc.tile_pool(name="small", bufs=3))
         latent = stack.enter_context(tc.tile_pool(name="latent", bufs=3))
-        work = stack.enter_context(tc.tile_pool(name="work", bufs=2))
+        work = stack.enter_context(tc.tile_pool(name="work", bufs=3))
         opool = stack.enter_context(tc.tile_pool(name="opool", bufs=3))
-        ps_ring = stack.enter_context(tc.psum_pool(name="ps_ring", bufs=1))
+        ps = stack.enter_context(tc.psum_pool(name="ps", bufs=1))
         stack.enter_context(tc.manual_schedule())
 
         ring_count = [0]
@@ -61,10 +62,17 @@ def tile_transformerdecoderblock_pa_t_kernel(
         def ring_bank(shape):
             slot = ring_count[0] % RING
             ring_count[0] += 1
-            return ps_ring.tile(shape, F32, name="ring%d" % slot)
+            return ps.tile(shape, F32, name="ring%d" % slot)
 
         ident = consts.tile([P, P], F32, name="ident")
         masks.make_identity(nc, ident[:])
+
+        zero = consts.tile([P, 1], F32, name="zero")
+        nc.vector.memset(zero[:], 0.0)
+        eps = consts.tile([P, 1], F32, name="eps")
+        nc.vector.tensor_scalar(out=eps[:], in0=zero[:], scalar1=EPS, scalar2=None, op0=ALU.add)
+        warm = consts.tile([P, 1], F32, name="warm")
+        nc.scalar.activation(out=warm[:], in_=zero[:], func=ACT.Abs_reciprocal_sqrt, bias=eps[:], scale=1.0)
 
         gain_bias = consts.tile([P, BRANCHES, 2, PACK], F32, name="gain_bias")
         vec_raw = consts.tile([P, BRANCHES, 2, 16], BF16, name="vec_raw")
@@ -75,8 +83,6 @@ def tile_transformerdecoderblock_pa_t_kernel(
                     in_=gain_bias_vecs[br][v].rearrange("(p t) -> p t", t=PACK),
                 )
         nc.gpsimd.tensor_copy(out=gain_bias[:], in_=vec_raw[:, :, :, 0:PACK])
-        neg_half = consts.tile([P, TILES], F32, name="neg_half")
-        nc.gpsimd.memset(neg_half[:], -0.5)
 
         def load_down(br):
             raw = wstage.tile([P, PACK, LATENT], BF16, name="down_raw%d" % br)
@@ -120,12 +126,16 @@ def tile_transformerdecoderblock_pa_t_kernel(
             )
             return grouped
 
-        def regroup_up(br, copy):
+        def regroup_up(br):
             width = OUT_BANKS[br] * BANK
             grouped = wstage.tile([P, width, PACK], BF16, name="up_grouped%d" % br, align_bytes=64)
-            copy(
+            nc.gpsimd.tensor_scalar(
                 out=grouped[:].rearrange("p (c i) j -> p c j i", i=4),
-                in_=up_raw[br][:].rearrange("p j (c i) -> p c j i", i=4),
+                in0=up_raw[br][:].rearrange("p j (c i) -> p c j i", i=4),
+                scalar1=1.0,
+                scalar2=0.0,
+                op0=ALU.mult,
+                op1=ALU.add,
             )
             return grouped
 
@@ -145,31 +155,31 @@ def tile_transformerdecoderblock_pa_t_kernel(
             return n_t
 
         def copy_tokens(half, n_t):
-            s, h = divmod(half, 2)
-            if h == 0:
-                n_grouped[s] = npool.tile([P, GROUP, PACK], BF16, name="n_grouped", align_bytes=64)
+            n_grouped[half] = npool.tile([P, HALF, PACK], BF16, name="n_grouped", align_bytes=64)
             n_words = (
-                n_grouped[s][:, h * HALF : (h + 1) * HALF, :]
+                n_grouped[half][:]
                 .rearrange("p w j -> p (w j)")
                 .bitcast(F32)
                 .rearrange("p (w u) -> p w u", u=2)
             )
             nc.scalar.copy(out=n_words, in_=n_t[:].rearrange("p u w -> p w u"))
 
-        def quantise_tokens(s):
-            n_codes[s] = npool.tile([P, GROUP], U32, name="n_codes", align_bytes=64)
-            n_scales[s] = npool.tile([P, GROUP], U8, name="n_scales", align_bytes=64)
+        def quantise_tokens(half):
+            s, h = divmod(half, 2)
+            if h == 0:
+                n_codes[s] = npool.tile([P, GROUP], U32, name="n_codes", align_bytes=64)
+                n_scales[s] = npool.tile([P, GROUP], U8, name="n_scales", align_bytes=64)
             nc.vector.quantize_mx(
-                out=n_codes[s][:].bitcast(FP8X4),
-                scales=n_scales[s][:],
-                in_=n_grouped[s][:].rearrange("p w j -> p (w j)"),
+                out=n_codes[s][:, h * HALF : (h + 1) * HALF].bitcast(FP8X4),
+                scales=n_scales[s][:, h * HALF : (h + 1) * HALF],
+                in_=n_grouped[half][:].rearrange("p w j -> p (w j)"),
             )
 
-        c_f32 = {}
+        sums = {}
+        c_norm = {}
         stats = {}
         mean_var = {}
         rstd = {}
-        neg_mean = {}
         planes = {}
         c_grouped = {}
         c_codes = {}
@@ -177,9 +187,9 @@ def tile_transformerdecoderblock_pa_t_kernel(
 
         def down_matmul(unit, j):
             s, br = divmod(unit, BRANCHES)
-            sums = ring_bank([P, LATENT])
+            sums[unit, j] = ps.tile([P, LATENT], F32, name="sums%d" % j)
             nc.tensor.matmul_mx(
-                out=sums[:],
+                out=sums[unit, j][:],
                 lhsT=n_codes[s][:, j * P : (j + 1) * P].bitcast(FP8X4),
                 lhsT_scale=n_scales[s][:, j * P : (j + 1) * P],
                 rhs=down_codes[br][:].bitcast(FP8X4),
@@ -187,41 +197,34 @@ def tile_transformerdecoderblock_pa_t_kernel(
                 start=True,
                 stop=True,
             )
-            return sums
 
-        def copy_sums(unit, j, sums):
-            if j == 0:
-                c_f32[unit] = latent.tile([P, TILES, LATENT], F32, name="c_f32")
-            nc.scalar.copy(out=c_f32[unit][:, j, :], in_=sums[:])
-
-        def token_stats(unit, j):
-            if j == 0:
-                stats[unit] = small.tile([P, TILES, 6], F32, name="stats")
-                mean_var[unit] = small.tile([P, TILES, 2], F32, name="mean_var")
-            nc.vector.bn_stats(out=stats[unit][:, j, :], in_=c_f32[unit][:, j, :])
-            nc.vector.bn_aggr(out=mean_var[unit][:, j, :], in_=stats[unit][:, j, :])
+        def token_stats(unit):
+            stats[unit] = small.tile([P, TILES, 6], F32, name="stats")
+            mean_var[unit] = small.tile([P, TILES, 2], F32, name="mean_var")
+            for j in range(TILES):
+                nc.vector.bn_stats(out=stats[unit][:, j, :], in_=sums[unit, j][:])
+            for j in range(TILES):
+                nc.vector.bn_aggr(out=mean_var[unit][:, j, :], in_=stats[unit][:, j, :])
 
         def reciprocal_std(unit):
-            var_eps = small.tile([P, TILES], F32, name="var_eps")
-            nc.gpsimd.tensor_scalar(
-                out=var_eps[:], in0=mean_var[unit][:, :, 1], scalar1=1.0, scalar2=EPS, op0=ALU.mult, op1=ALU.add
-            )
             rstd[unit] = small.tile([P, TILES], F32, name="rstd")
-            nc.gpsimd.tensor_tensor(out=rstd[unit][:], in0=var_eps[:], in1=neg_half[:], op=ALU.pow)
-
-        def negative_mean(unit):
-            neg_mean[unit] = small.tile([P, TILES], F32, name="neg_mean")
-            nc.vector.tensor_scalar(
-                out=neg_mean[unit][:], in0=mean_var[unit][:, :, 0], scalar1=-1.0, scalar2=None, op0=ALU.mult
+            nc.scalar.activation(
+                out=rstd[unit][:],
+                in_=mean_var[unit][:, :, 1],
+                func=ACT.Abs_reciprocal_sqrt,
+                bias=eps[:],
+                scale=1.0,
             )
 
-        def normalise(unit, j, engine):
-            engine.tensor_scalar(
-                out=c_f32[unit][:, j, :],
-                in0=c_f32[unit][:, j, :],
-                scalar1=neg_mean[unit][:, j : j + 1],
+        def normalise(unit, j):
+            if j == 0:
+                c_norm[unit] = latent.tile([P, TILES, LATENT], F32, name="c_norm")
+            nc.vector.tensor_scalar(
+                out=c_norm[unit][:, j, :],
+                in0=sums[unit, j][:],
+                scalar1=mean_var[unit][:, j, 0:1],
                 scalar2=rstd[unit][:, j : j + 1],
-                op0=ALU.add,
+                op0=ALU.subtract,
                 op1=ALU.mult,
             )
 
@@ -229,28 +232,33 @@ def tile_transformerdecoderblock_pa_t_kernel(
             x_t = ring_bank([P, GROUP])
             for j in range(TILES):
                 nc.tensor.transpose(
-                    x_t[:, j * P : (j + 1) * P], c_f32[unit][:, j, t * P : (t + 1) * P], ident[:]
+                    x_t[:, j * P : (j + 1) * P], c_norm[unit][:, j, t * P : (t + 1) * P], ident[:]
                 )
             return x_t
 
-        def gain_and_bias(unit, t, x_t):
+        def gain_and_bias(unit, t, x_t, on_vector):
             br = unit % BRANCHES
             if t == 0:
                 planes[unit] = work.tile([P, PACK, GROUP], BF16, name="planes")
-            nc.scalar.activation(
-                out=planes[unit][:, t, :],
-                in_=x_t[:],
-                func=ACT.Identity,
-                scale=gain_bias[:, br, 0, t : t + 1],
-                bias=gain_bias[:, br, 1, t : t + 1],
-            )
+            gain = gain_bias[:, br, 0, t : t + 1]
+            bias = gain_bias[:, br, 1, t : t + 1]
+            if on_vector:
+                nc.vector.tensor_scalar(
+                    out=planes[unit][:, t, :], in0=x_t[:], scalar1=gain, scalar2=bias, op0=ALU.mult, op1=ALU.add
+                )
+            else:
+                nc.scalar.activation(
+                    out=planes[unit][:, t, :], in_=x_t[:], func=ACT.Identity, scale=gain, bias=bias
+                )
 
-        def regroup_latent(unit):
+        def regroup_latent(unit, on_vector):
             c_grouped[unit] = work.tile([P, GROUP, PACK], BF16, name="c_grouped", align_bytes=64)
-            nc.vector.tensor_copy(
-                out=c_grouped[unit][:].rearrange("p (c i) t -> p c t i", i=4),
-                in_=planes[unit][:].rearrange("p t (c i) -> p c t i", i=4),
-            )
+            dst = c_grouped[unit][:].rearrange("p (c i) t -> p c t i", i=4)
+            src = planes[unit][:].rearrange("p t (c i) -> p c t i", i=4)
+            if on_vector:
+                nc.vector.tensor_copy(out=dst, in_=src)
+            else:
+                nc.gpsimd.tensor_scalar(out=dst, in0=src, scalar1=1.0, scalar2=0.0, op0=ALU.mult, op1=ALU.add)
 
         def quantise_latent(unit):
             br = unit % BRANCHES
@@ -276,73 +284,84 @@ def tile_transformerdecoderblock_pa_t_kernel(
             )
             return acc
 
-        def up_and_store(unit):
-            s, br = divmod(unit, BRANCHES)
-            bank = 0
-            for h in range(2):
-                result = opool.tile([P, HALF_TILES, OUT_BANKS[br] * BANK], F32, name="result%d" % br)
-                for jj in range(HALF_TILES):
-                    for n in range(OUT_BANKS[br]):
-                        acc = up_matmul(unit, h * HALF_TILES + jj, n)
-                        if bank % 2 == 0:
-                            nc.vector.tensor_copy(out=result[:, jj, n * BANK : (n + 1) * BANK], in_=acc[:])
-                        else:
-                            nc.scalar.copy(out=result[:, jj, n * BANK : (n + 1) * BANK], in_=acc[:])
-                        bank += 1
-                nc.sync.dma_start(out=out_views[br][2 * s + h], in_=result[:])
+        results = {}
+        pending = []
+
+        def emit_outputs(count, on_vector):
+            for i in range(min(count, len(pending))):
+                unit, j, n = pending.pop(0)
+                s, br = divmod(unit, BRANCHES)
+                h, jj = divmod(j, HALF_TILES)
+                if jj == 0 and n == 0:
+                    results[br] = opool.tile([P, HALF_TILES, OUT_BANKS[br] * BANK], F32, name="result%d" % br)
+                acc = up_matmul(unit, j, n)
+                dst = results[br][:, jj, n * BANK : (n + 1) * BANK]
+                if on_vector(i):
+                    nc.vector.tensor_copy(out=dst, in_=acc[:])
+                else:
+                    nc.scalar.copy(out=dst, in_=acc[:])
+                if jj == HALF_TILES - 1 and n == OUT_BANKS[br] - 1:
+                    nc.sync.dma_start(out=out_views[br][2 * s + h], in_=results[br][:])
 
         for half in range(2):
             copy_tokens(half, transpose_tokens(half))
         down_grouped = [regroup_down(0, nc.vector.tensor_copy), regroup_down(1, nc.scalar.copy)]
-        quantise_tokens(0)
+        for half in range(2):
+            quantise_tokens(half)
         down_codes = []
         down_scales = []
         up_codes = []
         up_scales = []
-        for br in range(BRANCHES):
+
+        def add_down(br):
             codes, scales = quantise_weight(down_grouped[br], LATENT, "down%d" % br)
             down_codes.append(codes)
             down_scales.append(scales)
 
+        def add_up(br):
+            codes, scales = quantise_weight(up_grouped[br], OUT_BANKS[br] * BANK, "up%d" % br)
+            up_codes.append(codes)
+            up_scales.append(scales)
+
+        add_down(0)
+        up_grouped = [regroup_up(br) for br in range(BRANCHES)]
+
         def unit_or_none(u):
             return u if 0 <= u < UNITS else None
 
-        for k in range(UNITS + 3):
+        for k in range(UNITS + 2):
             first = unit_or_none(k)
             second = unit_or_none(k - 1)
             third = unit_or_none(k - 2)
-            fourth = unit_or_none(k - 3)
             vector_free = first is None
 
-            if fourth is not None:
-                regroup_latent(fourth)
-            if k % 2 == 1 and (k + 1) // 2 < GROUPS:
-                quantise_tokens((k + 1) // 2)
-            if fourth is not None:
-                quantise_latent(fourth)
-            if second is not None:
-                negative_mean(second)
-                for j in range(TILES):
-                    normalise(second, j, nc.vector if vector_free else nc.gpsimd)
             if first is not None:
                 for j in range(TILES):
-                    copy_sums(first, j, down_matmul(first, j))
-                for j in range(TILES):
-                    token_stats(first, j)
-                reciprocal_std(first)
-            if k == 1 or k == 2:
-                br = k - 1
-                codes, scales = quantise_weight(
-                    regroup_up(br, nc.vector.tensor_copy), OUT_BANKS[br] * BANK, "up%d" % br
-                )
-                up_codes.append(codes)
-                up_scales.append(scales)
-            if third is not None:
-                for t in range(PACK):
-                    gain_and_bias(third, t, transpose_latent(third, t))
+                    down_matmul(first, j)
+                token_stats(first)
+            emit_outputs(PERIOD_BANKS // 2, lambda i: vector_free and i % 2 == 0)
+            if k + 2 < HALVES:
+                copy_tokens(k + 2, transpose_tokens(k + 2))
+            for t in range(PACK):
+                if second is not None:
+                    gain_and_bias(second, t, transpose_latent(second, t), vector_free and t % 2 == 0)
+                if t == 1 and first is not None:
+                    reciprocal_std(first)
+            if second is not None:
+                regroup_latent(second, vector_free)
+            if k + 2 < HALVES:
+                quantise_tokens(k + 2)
             if k == 0:
-                copy_tokens(2, transpose_tokens(2))
-            if k + 3 < HALVES:
-                copy_tokens(k + 3, transpose_tokens(k + 3))
-            if fourth is not None:
-                up_and_store(fourth)
+                add_down(1)
+            if 0 < k <= BRANCHES:
+                add_up(k - 1)
+            if third is not None:
+                quantise_latent(third)
+                pending.extend(
+                    [(third, j, n) for j in range(TILES) for n in range(OUT_BANKS[third % BRANCHES])]
+                )
+            if first is not None:
+                for j in range(TILES):
+                    normalise(first, j)
+            emit_outputs(PERIOD_BANKS // 2, lambda i: vector_free and i % 2 == 1)
+        emit_outputs(len(pending), lambda i: i % 2 == 0)

@@ -130,8 +130,8 @@ def tile_transformerdecoderblock_pa_t_kernel(
             width = OUT_BANKS[br] * BANK
             grouped = wstage.tile([P, width, PACK], BF16, name="up_grouped%d" % br, align_bytes=64)
             nc.gpsimd.tensor_scalar(
-                out=grouped[:].rearrange("p (c i) j -> p c j i", i=4),
-                in0=up_raw[br][:].rearrange("p j (c i) -> p c j i", i=4),
+                out=grouped[:],
+                in0=up_raw[br][:].rearrange("p j w -> p w j"),
                 scalar1=1.0,
                 scalar2=0.0,
                 op0=ALU.mult,
@@ -253,12 +253,20 @@ def tile_transformerdecoderblock_pa_t_kernel(
 
         def regroup_latent(unit, on_vector):
             c_grouped[unit] = work.tile([P, GROUP, PACK], BF16, name="c_grouped", align_bytes=64)
-            dst = c_grouped[unit][:].rearrange("p (c i) t -> p c t i", i=4)
-            src = planes[unit][:].rearrange("p t (c i) -> p c t i", i=4)
             if on_vector:
-                nc.vector.tensor_copy(out=dst, in_=src)
+                nc.vector.tensor_copy(
+                    out=c_grouped[unit][:].rearrange("p (c i) t -> p c t i", i=4),
+                    in_=planes[unit][:].rearrange("p t (c i) -> p c t i", i=4),
+                )
             else:
-                nc.gpsimd.tensor_scalar(out=dst, in0=src, scalar1=1.0, scalar2=0.0, op0=ALU.mult, op1=ALU.add)
+                nc.gpsimd.tensor_scalar(
+                    out=c_grouped[unit][:],
+                    in0=planes[unit][:].rearrange("p t w -> p w t"),
+                    scalar1=1.0,
+                    scalar2=0.0,
+                    op0=ALU.mult,
+                    op1=ALU.add,
+                )
 
         def quantise_latent(unit):
             br = unit % BRANCHES
@@ -335,18 +343,20 @@ def tile_transformerdecoderblock_pa_t_kernel(
             third = unit_or_none(k - 2)
             vector_free = first is None
 
-            if first is not None:
-                for j in range(TILES):
+            for j in range(TILES):
+                if first is not None:
                     down_matmul(first, j)
+                if j > 0:
+                    emit_outputs(1, lambda i: vector_free and j % 2 == 0)
+            if first is not None:
                 token_stats(first)
-            emit_outputs(PERIOD_BANKS // 2, lambda i: vector_free and i % 2 == 0)
             if k + 2 < HALVES:
                 copy_tokens(k + 2, transpose_tokens(k + 2))
-            for t in range(PACK):
-                if second is not None:
+            if first is not None:
+                reciprocal_std(first)
+            if second is not None:
+                for t in range(PACK):
                     gain_and_bias(second, t, transpose_latent(second, t), vector_free and t % 2 == 0)
-                if t == 1 and first is not None:
-                    reciprocal_std(first)
             if second is not None:
                 regroup_latent(second, vector_free)
             if k + 2 < HALVES:

@@ -28,7 +28,11 @@ BRANCHES = 2
 OUT_BANKS = (2, 1)
 UNITS = GROUPS * BRANCHES
 RING = 4
-PERIOD_BANKS = 6
+PAIRS = 2
+EARLY_UNITS = 1
+EARLY_TOKENS = (3, 5, 2)
+UP_PERIODS = (1, 3)
+PAIRS = 2
 FLOPS = 2 * TOKENS * 512 * (512 + 512 + 512 + 1024)
 
 
@@ -52,6 +56,7 @@ def tile_transformerdecoderblock_pa_t_kernel(
         npool = stack.enter_context(tc.tile_pool(name="npool", bufs=2))
         small = stack.enter_context(tc.tile_pool(name="small", bufs=3))
         latent = stack.enter_context(tc.tile_pool(name="latent", bufs=3))
+        ngroup = stack.enter_context(tc.tile_pool(name="ngroup", bufs=HALVES))
         work = stack.enter_context(tc.tile_pool(name="work", bufs=3))
         opool = stack.enter_context(tc.tile_pool(name="opool", bufs=3))
         ps = stack.enter_context(tc.psum_pool(name="ps", bufs=1))
@@ -102,10 +107,14 @@ def tile_transformerdecoderblock_pa_t_kernel(
             nc.sync.dma_start(out=raw[:], in_=up_w[br].rearrange("(p j) w -> p j w", j=PACK))
             return raw
 
-        x_tiles = [load_tokens(0)]
-        down_raw = [load_down(br) for br in range(BRANCHES)]
+        x_tiles = [xpool.tile([P, TILES, FEATURES], BF16, name="x0")]
+        nc.sync.dma_start(out=x_tiles[0][:, 0:HALF_TILES, :], in_=x_view[0][:, 0:HALF_TILES, :])
+        down_raw = [load_down(0)]
+        nc.sync.dma_start(out=x_tiles[0][:, HALF_TILES:TILES, :], in_=x_view[0][:, HALF_TILES:TILES, :])
+        down_raw.append(load_down(1))
+        up_raw = [load_up(0)]
         x_tiles.append(load_tokens(1))
-        up_raw = [load_up(br) for br in range(BRANCHES)]
+        up_raw.append(load_up(1))
         x_tiles.extend([load_tokens(s) for s in range(2, GROUPS)])
 
         def quantise_weight(grouped, width, name):
@@ -129,14 +138,15 @@ def tile_transformerdecoderblock_pa_t_kernel(
         def regroup_up(br):
             width = OUT_BANKS[br] * BANK
             grouped = wstage.tile([P, width, PACK], BF16, name="up_grouped%d" % br, align_bytes=64)
-            nc.gpsimd.tensor_scalar(
-                out=grouped[:],
-                in0=up_raw[br][:].rearrange("p j w -> p w j"),
-                scalar1=1.0,
-                scalar2=0.0,
-                op0=ALU.mult,
-                op1=ALU.add,
-            )
+            for c in range(0, width, P):
+                nc.gpsimd.tensor_scalar(
+                    out=grouped[:, c : c + P, :],
+                    in0=up_raw[br][:, :, c : c + P].rearrange("p j w -> p w j"),
+                    scalar1=1.0,
+                    scalar2=0.0,
+                    op0=ALU.mult,
+                    op1=ALU.add,
+                )
             return grouped
 
         n_grouped = {}
@@ -155,7 +165,7 @@ def tile_transformerdecoderblock_pa_t_kernel(
             return n_t
 
         def copy_tokens(half, n_t):
-            n_grouped[half] = npool.tile([P, HALF, PACK], BF16, name="n_grouped", align_bytes=64)
+            n_grouped[half] = ngroup.tile([P, HALF, PACK], BF16, name="n_grouped", align_bytes=64)
             n_words = (
                 n_grouped[half][:]
                 .rearrange("p w j -> p (w j)")
@@ -180,6 +190,7 @@ def tile_transformerdecoderblock_pa_t_kernel(
         stats = {}
         mean_var = {}
         rstd = {}
+        neg_shift = {}
         planes = {}
         c_grouped = {}
         c_codes = {}
@@ -198,32 +209,58 @@ def tile_transformerdecoderblock_pa_t_kernel(
                 stop=True,
             )
 
-        def token_stats(unit):
-            stats[unit] = small.tile([P, TILES, 6], F32, name="stats")
-            mean_var[unit] = small.tile([P, TILES, 2], F32, name="mean_var")
-            for j in range(TILES):
-                nc.vector.bn_stats(out=stats[unit][:, j, :], in_=sums[unit, j][:])
-            for j in range(TILES):
-                nc.vector.bn_aggr(out=mean_var[unit][:, j, :], in_=stats[unit][:, j, :])
+        def pair_tiles(pair):
+            return range(pair * TILES // PAIRS, (pair + 1) * TILES // PAIRS)
 
-        def reciprocal_std(unit):
-            rstd[unit] = small.tile([P, TILES], F32, name="rstd")
+        def token_stats(unit, j):
+            if j == 0:
+                stats[unit] = small.tile([P, TILES, 6], F32, name="stats")
+            nc.vector.bn_stats(out=stats[unit][:, j, :], in_=sums[unit, j][:])
+
+        def aggregate(unit, pair):
+            mean_var[unit, pair] = small.tile([P, TILES // PAIRS, 2], F32, name="mean_var%d" % pair)
+            for i, j in enumerate(pair_tiles(pair)):
+                nc.vector.bn_aggr(out=mean_var[unit, pair][:, i, :], in_=stats[unit][:, j, :])
+
+        def reciprocal_std(unit, pair):
+            rstd[unit, pair] = small.tile([P, TILES // PAIRS], F32, name="rstd%d" % pair)
             nc.scalar.activation(
-                out=rstd[unit][:],
-                in_=mean_var[unit][:, :, 1],
+                out=rstd[unit, pair][:],
+                in_=mean_var[unit, pair][:, :, 1],
                 func=ACT.Abs_reciprocal_sqrt,
                 bias=eps[:],
                 scale=1.0,
             )
 
-        def normalise(unit, j):
+        def shift(unit, pair):
+            neg_shift[unit, pair] = small.tile([P, TILES // PAIRS], F32, name="neg_shift")
+            nc.vector.scalar_tensor_tensor(
+                out=neg_shift[unit, pair][:],
+                in0=mean_var[unit, pair][:, :, 0],
+                scalar=-1.0,
+                in1=rstd[unit, pair][:],
+                op0=ALU.mult,
+                op1=ALU.mult,
+            )
+
+        def normalise(unit, j, on_scalar):
             if j == 0:
                 c_norm[unit] = latent.tile([P, TILES, LATENT], F32, name="c_norm")
+            pair, i = divmod(j, TILES // PAIRS)
+            if on_scalar:
+                nc.scalar.activation(
+                    out=c_norm[unit][:, j, :],
+                    in_=sums[unit, j][:],
+                    func=ACT.Identity,
+                    scale=rstd[unit, pair][:, i : i + 1],
+                    bias=neg_shift[unit, pair][:, i : i + 1],
+                )
+                return
             nc.vector.tensor_scalar(
                 out=c_norm[unit][:, j, :],
                 in0=sums[unit, j][:],
-                scalar1=mean_var[unit][:, j, 0:1],
-                scalar2=rstd[unit][:, j : j + 1],
+                scalar1=mean_var[unit, pair][:, i, 0:1],
+                scalar2=rstd[unit, pair][:, i : i + 1],
                 op0=ALU.subtract,
                 op1=ALU.mult,
             )
@@ -308,14 +345,17 @@ def tile_transformerdecoderblock_pa_t_kernel(
                     nc.vector.tensor_copy(out=dst, in_=acc[:])
                 else:
                     nc.scalar.copy(out=dst, in_=acc[:])
-                if jj == HALF_TILES - 1 and n == OUT_BANKS[br] - 1:
+                if n < OUT_BANKS[br] - 1:
+                    continue
+                if unit >= UNITS - 2:
+                    nc.sync.dma_start(out=out_views[br][2 * s + h][:, jj, :], in_=results[br][:, jj, :])
+                elif jj == HALF_TILES - 1:
                     nc.sync.dma_start(out=out_views[br][2 * s + h], in_=results[br][:])
 
         for half in range(2):
             copy_tokens(half, transpose_tokens(half))
         down_grouped = [regroup_down(0, nc.vector.tensor_copy), regroup_down(1, nc.scalar.copy)]
-        for half in range(2):
-            quantise_tokens(half)
+        quantise_tokens(0)
         down_codes = []
         down_scales = []
         up_codes = []
@@ -332,46 +372,72 @@ def tile_transformerdecoderblock_pa_t_kernel(
             up_scales.append(scales)
 
         add_down(0)
-        up_grouped = [regroup_up(br) for br in range(BRANCHES)]
+        quantise_tokens(1)
+        up_grouped = [regroup_up(0)]
 
-        def unit_or_none(u):
-            return u if 0 <= u < UNITS else None
+        halves_left = list(range(2, HALVES))
 
-        for k in range(UNITS + 2):
-            first = unit_or_none(k)
-            second = unit_or_none(k - 1)
-            third = unit_or_none(k - 2)
-            vector_free = first is None
+        def bring_tokens(count):
+            for i in range(min(count, len(halves_left))):
+                half = halves_left.pop(0)
+                copy_tokens(half, transpose_tokens(half))
 
+        def add_outputs(unit):
+            pending.extend([(unit, j, n) for j in range(TILES) for n in range(OUT_BANKS[unit % BRANCHES])])
+
+        on_scalar = lambda i: False
+        last = UNITS - 1
+
+        for k in range(UNITS):
             for j in range(TILES):
-                if first is not None:
-                    down_matmul(first, j)
-                if j > 0:
-                    emit_outputs(1, lambda i: vector_free and j % 2 == 0)
-            if first is not None:
-                token_stats(first)
-            if k + 2 < HALVES:
-                copy_tokens(k + 2, transpose_tokens(k + 2))
-            if first is not None:
-                reciprocal_std(first)
-            if second is not None:
-                for t in range(PACK):
-                    gain_and_bias(second, t, transpose_latent(second, t), vector_free and t % 2 == 0)
-            if second is not None:
-                regroup_latent(second, vector_free)
+                down_matmul(k, j)
+                if j < 2 and k < last:
+                    emit_outputs(1, on_scalar)
+            for j in range(3):
+                token_stats(k, j)
+            aggregate(k, 0)
+            token_stats(k, 3)
+            if k == 0:
+                bring_tokens(2)
+                add_down(1)
+            if k > 1:
+                quantise_latent(k - 2)
+            aggregate(k, 1)
+            if k > 0:
+                for t in range(2):
+                    gain_and_bias(k - 1, t, transpose_latent(k - 1, t), False)
+            reciprocal_std(k, 0)
+            if k < last:
+                emit_outputs(1, on_scalar)
+            if k > 1:
+                add_outputs(k - 2)
+            if k in UP_PERIODS:
+                add_up(UP_PERIODS.index(k))
             if k + 2 < HALVES:
                 quantise_tokens(k + 2)
-            if k == 0:
-                add_down(1)
-            if 0 < k <= BRANCHES:
-                add_up(k - 1)
-            if third is not None:
-                quantise_latent(third)
-                pending.extend(
-                    [(third, j, n) for j in range(TILES) for n in range(OUT_BANKS[third % BRANCHES])]
-                )
-            if first is not None:
-                for j in range(TILES):
-                    normalise(first, j)
-            emit_outputs(PERIOD_BANKS // 2, lambda i: vector_free and i % 2 == 1)
+            if k > 0:
+                gain_and_bias(k - 1, 2, transpose_latent(k - 1, 2), False)
+            reciprocal_std(k, 1)
+            if k < EARLY_UNITS:
+                shift(k, 1)
+            for j in range(TILES):
+                normalise(k, j, k < EARLY_UNITS and j >= TILES // 2)
+            if k > 0:
+                gain_and_bias(k - 1, 3, transpose_latent(k - 1, 3), False)
+                regroup_latent(k - 1, False)
+            if k == 1:
+                up_grouped.append(regroup_up(1))
+            emit_outputs(3 if k < last else 6, on_scalar)
+            bring_tokens(EARLY_TOKENS[k] if k < len(EARLY_TOKENS) else 1)
+
+        emit_outputs(len(pending), on_scalar)
+        quantise_latent(last - 1)
+        add_outputs(last - 1)
+        for t in range(PACK):
+            gain_and_bias(last, t, transpose_latent(last, t), t % 2 == 1)
+        regroup_latent(last, True)
+        emit_outputs(3, lambda i: i == 2)
+        quantise_latent(last)
+        emit_outputs(len(pending), lambda i: i % 3 == 2)
+        add_outputs(last)
         emit_outputs(len(pending), lambda i: i % 2 == 0)

@@ -28,9 +28,9 @@ BRANCHES = 2
 OUT_BANKS = (2, 1)
 UNITS = GROUPS * BRANCHES
 RING = 4
-PAIRS = 2
 EARLY_UNITS = 1
 EARLY_TOKENS = (3, 5, 2)
+LATE_UNITS = 4
 UP_PERIODS = (1, 3)
 PAIRS = 2
 FLOPS = 2 * TOKENS * 512 * (512 + 512 + 512 + 1024)
@@ -347,7 +347,7 @@ def tile_transformerdecoderblock_pa_t_kernel(
                     nc.scalar.copy(out=dst, in_=acc[:])
                 if n < OUT_BANKS[br] - 1:
                     continue
-                if unit >= UNITS - 2:
+                if unit >= UNITS - LATE_UNITS:
                     nc.sync.dma_start(out=out_views[br][2 * s + h][:, jj, :], in_=results[br][:, jj, :])
                 elif jj == HALF_TILES - 1:
                     nc.sync.dma_start(out=out_views[br][2 * s + h], in_=results[br][:])
@@ -407,8 +407,6 @@ def tile_transformerdecoderblock_pa_t_kernel(
                 for t in range(2):
                     gain_and_bias(k - 1, t, transpose_latent(k - 1, t), False)
             reciprocal_std(k, 0)
-            if k < last:
-                emit_outputs(1, on_scalar)
             if k > 1:
                 add_outputs(k - 2)
             if k in UP_PERIODS:
@@ -427,7 +425,7 @@ def tile_transformerdecoderblock_pa_t_kernel(
                 regroup_latent(k - 1, False)
             if k == 1:
                 up_grouped.append(regroup_up(1))
-            emit_outputs(3 if k < last else 6, on_scalar)
+            emit_outputs(4 if k < last else 6, on_scalar)
             bring_tokens(EARLY_TOKENS[k] if k < len(EARLY_TOKENS) else 1)
 
         emit_outputs(len(pending), on_scalar)

@@ -28,9 +28,9 @@ BRANCHES = 2
 OUT_BANKS = (2, 1)
 UNITS = GROUPS * BRANCHES
 RING = 4
-EARLY_UNITS = 1
-EARLY_TOKENS = (3, 5, 2)
 LATE_UNITS = 4
+TOKENS_MID = {0: 2, 1: 1}
+TOKENS_END = {0: 2, 1: 5, 2: 2}
 UP_PERIODS = (1, 3)
 PAIRS = 2
 FLOPS = 2 * TOKENS * 512 * (512 + 512 + 512 + 1024)
@@ -108,14 +108,15 @@ def tile_transformerdecoderblock_pa_t_kernel(
             return raw
 
         x_tiles = [xpool.tile([P, TILES, FEATURES], BF16, name="x0")]
-        nc.sync.dma_start(out=x_tiles[0][:, 0:HALF_TILES, :], in_=x_view[0][:, 0:HALF_TILES, :])
+        nc.sync.dma_start(out=x_tiles[0][:, 0:1, :], in_=x_view[0][:, 0:1, :])
         down_raw = [load_down(0)]
-        nc.sync.dma_start(out=x_tiles[0][:, HALF_TILES:TILES, :], in_=x_view[0][:, HALF_TILES:TILES, :])
+        nc.sync.dma_start(out=x_tiles[0][:, 1:TILES, :], in_=x_view[0][:, 1:TILES, :])
         down_raw.append(load_down(1))
-        up_raw = [load_up(0)]
         x_tiles.append(load_tokens(1))
+        up_raw = [load_up(0)]
+        x_tiles.extend([load_tokens(s) for s in (2, 3)])
         up_raw.append(load_up(1))
-        x_tiles.extend([load_tokens(s) for s in range(2, GROUPS)])
+        x_tiles.extend([load_tokens(s) for s in range(4, GROUPS)])
 
         def quantise_weight(grouped, width, name):
             codes = consts.tile([P, width], U32, name=name + "_codes", align_bytes=64)
@@ -185,12 +186,37 @@ def tile_transformerdecoderblock_pa_t_kernel(
                 in_=n_grouped[half][:].rearrange("p w j -> p (w j)"),
             )
 
+        def copy_tile(tile):
+            if tile == 0:
+                n_grouped[0] = ngroup.tile([P, HALF, PACK], BF16, name="n_grouped", align_bytes=64)
+            n_t = ring_bank([P, 2, P])
+            x_words = x_tiles[0][:, tile, :].bitcast(F32)
+            for u in range(2):
+                nc.tensor.transpose(n_t[:, u, :], x_words[:, u * P : (u + 1) * P], ident[:])
+            n_words = (
+                n_grouped[0][:, tile * P : (tile + 1) * P, :]
+                .rearrange("p w j -> p (w j)")
+                .bitcast(F32)
+                .rearrange("p (w u) -> p w u", u=2)
+            )
+            nc.scalar.copy(out=n_words, in_=n_t[:].rearrange("p u w -> p w u"))
+
+        def quantise_tile(tile):
+            if tile == 0:
+                n_codes[0] = npool.tile([P, GROUP], U32, name="n_codes", align_bytes=64)
+                n_scales[0] = npool.tile([P, GROUP], U8, name="n_scales", align_bytes=64)
+            cols = slice(tile * P, (tile + 1) * P)
+            nc.vector.quantize_mx(
+                out=n_codes[0][:, cols].bitcast(FP8X4),
+                scales=n_scales[0][:, cols],
+                in_=n_grouped[0][:, cols, :].rearrange("p w j -> p (w j)"),
+            )
+
         sums = {}
         c_norm = {}
         stats = {}
         mean_var = {}
         rstd = {}
-        neg_shift = {}
         planes = {}
         c_grouped = {}
         c_codes = {}
@@ -232,30 +258,10 @@ def tile_transformerdecoderblock_pa_t_kernel(
                 scale=1.0,
             )
 
-        def shift(unit, pair):
-            neg_shift[unit, pair] = small.tile([P, TILES // PAIRS], F32, name="neg_shift")
-            nc.vector.scalar_tensor_tensor(
-                out=neg_shift[unit, pair][:],
-                in0=mean_var[unit, pair][:, :, 0],
-                scalar=-1.0,
-                in1=rstd[unit, pair][:],
-                op0=ALU.mult,
-                op1=ALU.mult,
-            )
-
-        def normalise(unit, j, on_scalar):
+        def normalise(unit, j):
             if j == 0:
                 c_norm[unit] = latent.tile([P, TILES, LATENT], F32, name="c_norm")
             pair, i = divmod(j, TILES // PAIRS)
-            if on_scalar:
-                nc.scalar.activation(
-                    out=c_norm[unit][:, j, :],
-                    in_=sums[unit, j][:],
-                    func=ACT.Identity,
-                    scale=rstd[unit, pair][:, i : i + 1],
-                    bias=neg_shift[unit, pair][:, i : i + 1],
-                )
-                return
             nc.vector.tensor_scalar(
                 out=c_norm[unit][:, j, :],
                 in0=sums[unit, j][:],
@@ -352,10 +358,10 @@ def tile_transformerdecoderblock_pa_t_kernel(
                 elif jj == HALF_TILES - 1:
                     nc.sync.dma_start(out=out_views[br][2 * s + h], in_=results[br][:])
 
-        for half in range(2):
-            copy_tokens(half, transpose_tokens(half))
+        for tile in range(HALF_TILES):
+            copy_tile(tile)
+        copy_tokens(1, transpose_tokens(1))
         down_grouped = [regroup_down(0, nc.vector.tensor_copy), regroup_down(1, nc.scalar.copy)]
-        quantise_tokens(0)
         down_codes = []
         down_scales = []
         up_codes = []
@@ -371,7 +377,9 @@ def tile_transformerdecoderblock_pa_t_kernel(
             up_codes.append(codes)
             up_scales.append(scales)
 
+        quantise_tile(0)
         add_down(0)
+        quantise_tile(1)
         quantise_tokens(1)
         up_grouped = [regroup_up(0)]
 
@@ -398,7 +406,7 @@ def tile_transformerdecoderblock_pa_t_kernel(
             aggregate(k, 0)
             token_stats(k, 3)
             if k == 0:
-                bring_tokens(2)
+                bring_tokens(TOKENS_MID[k])
                 add_down(1)
             if k > 1:
                 quantise_latent(k - 2)
@@ -406,6 +414,8 @@ def tile_transformerdecoderblock_pa_t_kernel(
             if k > 0:
                 for t in range(2):
                     gain_and_bias(k - 1, t, transpose_latent(k - 1, t), False)
+            if k == 1:
+                bring_tokens(TOKENS_MID[k])
             reciprocal_std(k, 0)
             if k > 1:
                 add_outputs(k - 2)
@@ -416,19 +426,17 @@ def tile_transformerdecoderblock_pa_t_kernel(
             if k > 0:
                 gain_and_bias(k - 1, 2, transpose_latent(k - 1, 2), False)
             reciprocal_std(k, 1)
-            if k < EARLY_UNITS:
-                shift(k, 1)
             for j in range(TILES):
-                normalise(k, j, k < EARLY_UNITS and j >= TILES // 2)
+                normalise(k, j)
             if k > 0:
                 gain_and_bias(k - 1, 3, transpose_latent(k - 1, 3), False)
                 regroup_latent(k - 1, False)
             if k == 1:
                 up_grouped.append(regroup_up(1))
-            emit_outputs(4 if k < last else 6, on_scalar)
-            bring_tokens(EARLY_TOKENS[k] if k < len(EARLY_TOKENS) else 1)
+            emit_outputs(4, on_scalar)
+            bring_tokens(TOKENS_END.get(k, 1))
 
-        emit_outputs(len(pending), on_scalar)
+        emit_outputs(len(pending), lambda i: i % 2 == 1)
         quantise_latent(last - 1)
         add_outputs(last - 1)
         for t in range(PACK):

from contextlib import ExitStack

import concourse.masks as masks
import concourse.mybir as mybir

F32 = mybir.dt.float32
BF16 = mybir.dt.bfloat16
U32 = mybir.dt.uint32
U8 = mybir.dt.uint8
FP8X4 = mybir.dt.float8_e4m3fn_x4
ACT = mybir.ActivationFunctionType
ALU = mybir.AluOpType

P = 128
PACK = 4
FEATURES = 512
LATENT = 512
TOKENS = 4096
TILES = 4
GROUP = TILES * P
GROUPS = TOKENS // GROUP
HALF_TILES = TILES // 2
HALF = HALF_TILES * P
HALVES = 2 * GROUPS
BANK = 512
EPS = 1e-5
BRANCHES = 2
OUT_BANKS = (2, 1)
UNITS = GROUPS * BRANCHES
RING = 4
LATE_UNITS = 4
TOKENS_MID = {0: 2, 1: 1}
TOKENS_END = {0: 2, 1: 5, 2: 2}
UP_PERIODS = (1, 3)
PAIRS = 2
FLOPS = 2 * TOKENS * 512 * (512 + 512 + 512 + 1024)


def tile_transformerdecoderblock_pa_t_kernel(
    tc, normed, W_dq, q_ln_g, q_ln_b, W_uq, W_dkv, kv_ln_g, kv_ln_b, W_ukv, out_0, out_1
):
    nc = tc.nc
    down_w = (W_dkv, W_dq)
    up_w = (W_ukv, W_uq)
    gain_bias_vecs = ((kv_ln_g, kv_ln_b), (q_ln_g, q_ln_b))
    x_view = normed.flatten_outer_dims().rearrange("(p s j) d -> s p j d", s=GROUPS, j=TILES)
    out_views = (
        out_1.flatten_outer_dims().rearrange("(p h j) d -> h p j d", h=HALVES, j=HALF_TILES),
        out_0.flatten_outer_dims().rearrange("(p h j) d -> h p j d", h=HALVES, j=HALF_TILES),
    )

    with ExitStack() as stack:
        consts = stack.enter_context(tc.tile_pool(name="consts", bufs=1))
        wstage = stack.enter_context(tc.tile_pool(name="wstage", bufs=1))
        xpool = stack.enter_context(tc.tile_pool(name="xpool", bufs=1))
        npool = stack.enter_context(tc.tile_pool(name="npool", bufs=2))
        small = stack.enter_context(tc.tile_pool(name="small", bufs=3))
        latent = stack.enter_context(tc.tile_pool(name="latent", bufs=3))
        ngroup = stack.enter_context(tc.tile_pool(name="ngroup", bufs=HALVES))
        work = stack.enter_context(tc.tile_pool(name="work", bufs=3))
        opool = stack.enter_context(tc.tile_pool(name="opool", bufs=3))
        ps = stack.enter_context(tc.psum_pool(name="ps", bufs=1))
        stack.enter_context(tc.manual_schedule())

        ring_count = [0]

        def ring_bank(shape):
            slot = ring_count[0] % RING
            ring_count[0] += 1
            return ps.tile(shape, F32, name="ring%d" % slot)

        ident = consts.tile([P, P], F32, name="ident")
        masks.make_identity(nc, ident[:])

        zero = consts.tile([P, 1], F32, name="zero")
        nc.vector.memset(zero[:], 0.0)
        eps = consts.tile([P, 1], F32, name="eps")
        nc.vector.tensor_scalar(out=eps[:], in0=zero[:], scalar1=EPS, scalar2=None, op0=ALU.add)
        warm = consts.tile([P, 1], F32, name="warm")
        nc.scalar.activation(out=warm[:], in_=zero[:], func=ACT.Abs_reciprocal_sqrt, bias=eps[:], scale=1.0)

        gain_bias = consts.tile([P, BRANCHES, 2, PACK], F32, name="gain_bias")
        vec_raw = consts.tile([P, BRANCHES, 2, 16], BF16, name="vec_raw")
        for br in range(BRANCHES):
            for v in range(2):
                nc.scalar.dma_start(
                    out=vec_raw[:, br, v, 0:PACK],
                    in_=gain_bias_vecs[br][v].rearrange("(p t) -> p t", t=PACK),
                )
        nc.gpsimd.tensor_copy(out=gain_bias[:], in_=vec_raw[:, :, :, 0:PACK])

        def load_down(br):
            raw = wstage.tile([P, PACK, LATENT], BF16, name="down_raw%d" % br)
            nc.sync.dma_start(
                out=raw[:].rearrange("q (u e) c -> q u e c", u=2),
                in_=down_w[br].rearrange("(u q e) c -> q u e c", u=2, e=2),
            )
            return raw

        def load_tokens(s):
            x = xpool.tile([P, TILES, FEATURES], BF16, name="x%d" % s)
            nc.sync.dma_start(out=x[:], in_=x_view[s])
            return x

        def load_up(br):
            raw = wstage.tile([P, PACK, OUT_BANKS[br] * BANK], BF16, name="up_raw%d" % br)
            nc.sync.dma_start(out=raw[:], in_=up_w[br].rearrange("(p j) w -> p j w", j=PACK))
            return raw

        x_tiles = [xpool.tile([P, TILES, FEATURES], BF16, name="x0")]
        nc.sync.dma_start(out=x_tiles[0][:, 0:1, :], in_=x_view[0][:, 0:1, :])
        down_raw = [load_down(0)]
        nc.sync.dma_start(out=x_tiles[0][:, 1:TILES, :], in_=x_view[0][:, 1:TILES, :])
        down_raw.append(load_down(1))
        x_tiles.append(load_tokens(1))
        up_raw = [load_up(0)]
        x_tiles.extend([load_tokens(s) for s in (2, 3)])
        up_raw.append(load_up(1))
        x_tiles.extend([load_tokens(s) for s in range(4, GROUPS)])

        def quantise_weight(grouped, width, name):
            codes = consts.tile([P, width], U32, name=name + "_codes", align_bytes=64)
            scales = consts.tile([P, width], U8, name=name + "_scales", align_bytes=64)
            nc.vector.quantize_mx(
                out=codes[:].bitcast(FP8X4),
                scales=scales[:],
                in_=grouped[:].rearrange("k c j -> k (c j)"),
            )
            return codes, scales

        def regroup_down(br, copy):
            grouped = wstage.tile([P, LATENT, PACK], BF16, name="down_grouped%d" % br, align_bytes=64)
            copy(
                out=grouped[:].rearrange("k (t p) j -> k t p j", t=PACK),
                in_=down_raw[br][:].rearrange("k j (p t) -> k t p j", t=PACK),
            )
            return grouped

        def regroup_up(br):
            width = OUT_BANKS[br] * BANK
            grouped = wstage.tile([P, width, PACK], BF16, name="up_grouped%d" % br, align_bytes=64)
            for c in range(0, width, P):
                nc.gpsimd.tensor_scalar(
                    out=grouped[:, c : c + P, :],
                    in0=up_raw[br][:, :, c : c + P].rearrange("p j w -> p w j"),
                    scalar1=1.0,
                    scalar2=0.0,
                    op0=ALU.mult,
                    op1=ALU.add,
                )
            return grouped

        n_grouped = {}
        n_codes = {}
        n_scales = {}

        def transpose_tokens(half):
            s, h = divmod(half, 2)
            n_t = ring_bank([P, 2, HALF])
            for jj in range(HALF_TILES):
                x_words = x_tiles[s][:, HALF_TILES * h + jj, :].bitcast(F32)
                for u in range(2):
                    nc.tensor.transpose(
                        n_t[:, u, jj * P : (jj + 1) * P], x_words[:, u * P : (u + 1) * P], ident[:]
                    )
            return n_t

        def copy_tokens(half, n_t):
            n_grouped[half] = ngroup.tile([P, HALF, PACK], BF16, name="n_grouped", align_bytes=64)
            n_words = (
                n_grouped[half][:]
                .rearrange("p w j -> p (w j)")
                .bitcast(F32)
                .rearrange("p (w u) -> p w u", u=2)
            )
            nc.scalar.copy(out=n_words, in_=n_t[:].rearrange("p u w -> p w u"))

        def quantise_tokens(half):
            s, h = divmod(half, 2)
            if h == 0:
                n_codes[s] = npool.tile([P, GROUP], U32, name="n_codes", align_bytes=64)
                n_scales[s] = npool.tile([P, GROUP], U8, name="n_scales", align_bytes=64)
            nc.vector.quantize_mx(
                out=n_codes[s][:, h * HALF : (h + 1) * HALF].bitcast(FP8X4),
                scales=n_scales[s][:, h * HALF : (h + 1) * HALF],
                in_=n_grouped[half][:].rearrange("p w j -> p (w j)"),
            )

        def copy_tile(tile):
            if tile == 0:
                n_grouped[0] = ngroup.tile([P, HALF, PACK], BF16, name="n_grouped", align_bytes=64)
            n_t = ring_bank([P, 2, P])
            x_words = x_tiles[0][:, tile, :].bitcast(F32)
            for u in range(2):
                nc.tensor.transpose(n_t[:, u, :], x_words[:, u * P : (u + 1) * P], ident[:])
            n_words = (
                n_grouped[0][:, tile * P : (tile + 1) * P, :]
                .rearrange("p w j -> p (w j)")
                .bitcast(F32)
                .rearrange("p (w u) -> p w u", u=2)
            )
            nc.scalar.copy(out=n_words, in_=n_t[:].rearrange("p u w -> p w u"))

        def quantise_tile(tile):
            if tile == 0:
                n_codes[0] = npool.tile([P, GROUP], U32, name="n_codes", align_bytes=64)
                n_scales[0] = npool.tile([P, GROUP], U8, name="n_scales", align_bytes=64)
            cols = slice(tile * P, (tile + 1) * P)
            nc.vector.quantize_mx(
                out=n_codes[0][:, cols].bitcast(FP8X4),
                scales=n_scales[0][:, cols],
                in_=n_grouped[0][:, cols, :].rearrange("p w j -> p (w j)"),
            )

        sums = {}
        c_norm = {}
        stats = {}
        mean_var = {}
        rstd = {}
        planes = {}
        c_grouped = {}
        c_codes = {}
        c_scales = {}

        def down_matmul(unit, j):
            s, br = divmod(unit, BRANCHES)
            sums[unit, j] = ps.tile([P, LATENT], F32, name="sums%d" % j)
            nc.tensor.matmul_mx(
                out=sums[unit, j][:],
                lhsT=n_codes[s][:, j * P : (j + 1) * P].bitcast(FP8X4),
                lhsT_scale=n_scales[s][:, j * P : (j + 1) * P],
                rhs=down_codes[br][:].bitcast(FP8X4),
                rhs_scale=down_scales[br][:],
                start=True,
                stop=True,
            )

        def pair_tiles(pair):
            return range(pair * TILES // PAIRS, (pair + 1) * TILES // PAIRS)

        def token_stats(unit, j):
            if j == 0:
                stats[unit] = small.tile([P, TILES, 6], F32, name="stats")
            nc.vector.bn_stats(out=stats[unit][:, j, :], in_=sums[unit, j][:])

        def aggregate(unit, pair):
            mean_var[unit, pair] = small.tile([P, TILES // PAIRS, 2], F32, name="mean_var%d" % pair)
            for i, j in enumerate(pair_tiles(pair)):
                nc.vector.bn_aggr(out=mean_var[unit, pair][:, i, :], in_=stats[unit][:, j, :])

        def reciprocal_std(unit, pair):
            rstd[unit, pair] = small.tile([P, TILES // PAIRS], F32, name="rstd%d" % pair)
            nc.scalar.activation(
                out=rstd[unit, pair][:],
                in_=mean_var[unit, pair][:, :, 1],
                func=ACT.Abs_reciprocal_sqrt,
                bias=eps[:],
                scale=1.0,
            )

        def normalise(unit, j):
            if j == 0:
                c_norm[unit] = latent.tile([P, TILES, LATENT], F32, name="c_norm")
            pair, i = divmod(j, TILES // PAIRS)
            nc.vector.tensor_scalar(
                out=c_norm[unit][:, j, :],
                in0=sums[unit, j][:],
                scalar1=mean_var[unit, pair][:, i, 0:1],
                scalar2=rstd[unit, pair][:, i : i + 1],
                op0=ALU.subtract,
                op1=ALU.mult,
            )

        def transpose_latent(unit, t):
            x_t = ring_bank([P, GROUP])
            for j in range(TILES):
                nc.tensor.transpose(
                    x_t[:, j * P : (j + 1) * P], c_norm[unit][:, j, t * P : (t + 1) * P], ident[:]
                )
            return x_t

        def gain_and_bias(unit, t, x_t, on_vector):
            br = unit % BRANCHES
            if t == 0:
                planes[unit] = work.tile([P, PACK, GROUP], BF16, name="planes")
            gain = gain_bias[:, br, 0, t : t + 1]
            bias = gain_bias[:, br, 1, t : t + 1]
            if on_vector:
                nc.vector.tensor_scalar(
                    out=planes[unit][:, t, :], in0=x_t[:], scalar1=gain, scalar2=bias, op0=ALU.mult, op1=ALU.add
                )
            else:
                nc.scalar.activation(
                    out=planes[unit][:, t, :], in_=x_t[:], func=ACT.Identity, scale=gain, bias=bias
                )

        def regroup_latent(unit, on_vector):
            c_grouped[unit] = work.tile([P, GROUP, PACK], BF16, name="c_grouped", align_bytes=64)
            if on_vector:
                nc.vector.tensor_copy(
                    out=c_grouped[unit][:].rearrange("p (c i) t -> p c t i", i=4),
                    in_=planes[unit][:].rearrange("p t (c i) -> p c t i", i=4),
                )
            else:
                nc.gpsimd.tensor_scalar(
                    out=c_grouped[unit][:],
                    in0=planes[unit][:].rearrange("p t w -> p w t"),
                    scalar1=1.0,
                    scalar2=0.0,
                    op0=ALU.mult,
                    op1=ALU.add,
                )

        def quantise_latent(unit):
            br = unit % BRANCHES
            c_codes[unit] = work.tile([P, GROUP], U32, name="c_codes%d" % br, align_bytes=64)
            c_scales[unit] = work.tile([P, GROUP], U8, name="c_scales%d" % br, align_bytes=64)
            nc.vector.quantize_mx(
                out=c_codes[unit][:].bitcast(FP8X4),
                scales=c_scales[unit][:],
                in_=c_grouped[unit][:].rearrange("p w t -> p (w t)"),
            )

        def up_matmul(unit, j, n):
            br = unit % BRANCHES
            acc = ring_bank([P, BANK])
            nc.tensor.matmul_mx(
                out=acc[:],
                lhsT=c_codes[unit][:, j * P : (j + 1) * P].bitcast(FP8X4),
                lhsT_scale=c_scales[unit][:, j * P : (j + 1) * P],
                rhs=up_codes[br][:, n * BANK : (n + 1) * BANK].bitcast(FP8X4),
                rhs_scale=up_scales[br][:, n * BANK : (n + 1) * BANK],
                start=True,
                stop=True,
            )
            return acc

        results = {}
        pending = []

        def emit_outputs(count, on_vector):
            for i in range(min(count, len(pending))):
                unit, j, n = pending.pop(0)
                s, br = divmod(unit, BRANCHES)
                h, jj = divmod(j, HALF_TILES)
                if jj == 0 and n == 0:
                    results[br] = opool.tile([P, HALF_TILES, OUT_BANKS[br] * BANK], F32, name="result%d" % br)
                acc = up_matmul(unit, j, n)
                dst = results[br][:, jj, n * BANK : (n + 1) * BANK]
                if on_vector(i):
                    nc.vector.tensor_copy(out=dst, in_=acc[:])
                else:
                    nc.scalar.copy(out=dst, in_=acc[:])
                if n < OUT_BANKS[br] - 1:
                    continue
                if unit >= UNITS - LATE_UNITS:
                    nc.sync.dma_start(out=out_views[br][2 * s + h][:, jj, :], in_=results[br][:, jj, :])
                elif jj == HALF_TILES - 1:
                    nc.sync.dma_start(out=out_views[br][2 * s + h], in_=results[br][:])

        for tile in range(HALF_TILES):
            copy_tile(tile)
        copy_tokens(1, transpose_tokens(1))
        down_grouped = [regroup_down(0, nc.vector.tensor_copy), regroup_down(1, nc.scalar.copy)]
        down_codes = []
        down_scales = []
        up_codes = []
        up_scales = []

        def add_down(br):
            codes, scales = quantise_weight(down_grouped[br], LATENT, "down%d" % br)
            down_codes.append(codes)
            down_scales.append(scales)

        def add_up(br):
            codes, scales = quantise_weight(up_grouped[br], OUT_BANKS[br] * BANK, "up%d" % br)
            up_codes.append(codes)
            up_scales.append(scales)

        quantise_tile(0)
        add_down(0)
        quantise_tile(1)
        quantise_tokens(1)
        up_grouped = [regroup_up(0)]

        halves_left = list(range(2, HALVES))

        def bring_tokens(count):
            for i in range(min(count, len(halves_left))):
                half = halves_left.pop(0)
                copy_tokens(half, transpose_tokens(half))

        def add_outputs(unit):
            pending.extend([(unit, j, n) for j in range(TILES) for n in range(OUT_BANKS[unit % BRANCHES])])

        on_scalar = lambda i: False
        last = UNITS - 1

        for k in range(UNITS):
            for j in range(TILES):
                down_matmul(k, j)
                if j < 2 and k < last:
                    emit_outputs(1, on_scalar)
            for j in range(3):
                token_stats(k, j)
            aggregate(k, 0)
            token_stats(k, 3)
            if k == 0:
                bring_tokens(TOKENS_MID[k])
                add_down(1)
            if k > 1:
                quantise_latent(k - 2)
            aggregate(k, 1)
            if k > 0:
                for t in range(2):
                    gain_and_bias(k - 1, t, transpose_latent(k - 1, t), False)
            if k == 1:
                bring_tokens(TOKENS_MID[k])
            reciprocal_std(k, 0)
            if k > 1:
                add_outputs(k - 2)
            if k in UP_PERIODS:
                add_up(UP_PERIODS.index(k))
            if k + 2 < HALVES:
                quantise_tokens(k + 2)
            if k > 0:
                gain_and_bias(k - 1, 2, transpose_latent(k - 1, 2), False)
            reciprocal_std(k, 1)
            for j in range(TILES):
                normalise(k, j)
            if k > 0:
                gain_and_bias(k - 1, 3, transpose_latent(k - 1, 3), False)
                regroup_latent(k - 1, False)
            if k == 1:
                up_grouped.append(regroup_up(1))
            emit_outputs(4, on_scalar)
            bring_tokens(TOKENS_END.get(k, 1))

        emit_outputs(len(pending), lambda i: i % 2 == 1)
        quantise_latent(last - 1)
        add_outputs(last - 1)
        for t in range(PACK):
            gain_and_bias(last, t, transpose_latent(last, t), t % 2 == 1)
        regroup_latent(last, True)
        emit_outputs(3, lambda i: i == 2)
        quantise_latent(last)
        emit_outputs(len(pending), lambda i: i % 3 == 2)
        add_outputs(last)
        emit_outputs(len(pending), lambda i: i % 2 == 0)
